import numpy as np
import ml_dtypes


def mxq(x, axis, fmt="e4m3"):
    dtype, down = {"e4m3": (ml_dtypes.float8_e4m3fn, 7), "e5m2": (ml_dtypes.float8_e5m2, 14)}[fmt]
    v = np.moveaxis(np.asarray(x, np.float32).astype(ml_dtypes.bfloat16).astype(np.float64), axis, -1)
    blocks = v.reshape(v.shape[:-1] + (-1, 32))
    amax = np.abs(blocks).max(-1, keepdims=True)
    byte = np.maximum(np.where(amax > 0, np.frexp(amax)[1] - 1 + 127, 0) - down, 1)
    scale = np.exp2(byte - 127.0)
    codes = (blocks / scale).astype(np.float32).astype(dtype).astype(np.float64)
    return np.moveaxis((codes * scale).reshape(v.shape), -1, axis)


WIDE = False


def mx_kscale(k):
    if not WIDE:
        return np.ones(k)
    levels = np.array([10, -10, 5, -5, 0])
    if k % 512:
        return np.exp2(np.random.permutation(np.resize(levels, k // 32))).repeat(32)
    a = np.empty((k // 512, 16))
    for p in range(k // 512):
        a[p, :8] = np.random.permutation(np.resize(levels, 8))
        for g in range(8):
            far = levels[np.abs(levels - a[p, g]) >= 10]
            a[p, g + 8] = far[np.random.randint(len(far))]
    return np.exp2(a.ravel()).repeat(32)


BF16 = ml_dtypes.bfloat16


def bf(x):
    return np.asarray(x, np.float32).astype(BF16)


def f64(x):
    return np.asarray(x).astype(np.float64)


B, M, H_ENC, N, H_DEC = 8192, 512, 512, 128, 128
SNR = 25.0
NOISE_STD = float(np.sqrt(1.0 / (2.0 * 10.0 ** (SNR / 10.0))))


def setup_inputs():
    s = mx_kscale(M)
    t = mx_kscale(H_ENC)
    theta = np.random.uniform(0.3, 1.2)
    return {"x": bf(np.random.standard_normal((B, M)) * s),
            "noise": bf(np.random.standard_normal((B, N)) * NOISE_STD),
            "h": bf(np.array([np.cos(theta), np.sin(theta)])),
            "W1": bf(np.random.standard_normal((H_ENC, M)) / np.sqrt(M) / s[None, :] * t[:, None]),
            "b1": bf(np.random.standard_normal(H_ENC) * 0.3 * t),
            "W2": bf(np.random.standard_normal((N, H_ENC)) / np.sqrt(H_ENC) / t[None, :]),
            "b2": bf(np.random.standard_normal(N) * 0.3)}


def reference(x, noise, h, W1, b1, W2, b2):
    h = f64(h)
    a = np.maximum(f64(bf(mxq(f64(x), 1, "e4m3") @ mxq(f64(W1), 1, "e4m3").T)) + f64(b1), 0.0)
    z = (mxq(a, 1, "e4m3") @ mxq(f64(W2), 1, "e4m3").T) + f64(b2)
    scale = np.sqrt(N * 0.5)
    z = scale * z / np.linalg.norm(z, axis=1, keepdims=True)
    zc = z.reshape(B, N // 2, 2)
    yr = zc[..., 0] * h[0] - zc[..., 1] * h[1]
    yi = zc[..., 0] * h[1] + zc[..., 1] * h[0]
    y = np.stack([yr, yi], axis=-1).reshape(B, N)
    return y + f64(noise)

@@ -1,0 +1,313 @@
+from contextlib import ExitStack
+
+import concourse.mybir as mybir
+from concourse.masks import make_identity
+
+FLOPS = 2 * 8192 * 512 * 512 + 2 * 8192 * 512 * 128
+
+F32 = mybir.dt.float32
+BF16 = mybir.dt.bfloat16
+U32 = mybir.dt.uint32
+U8 = mybir.dt.uint8
+FP8X4 = mybir.dt.float8_e4m3fn_x4
+ACT = mybir.ActivationFunctionType
+ALU = mybir.AluOpType
+AX = mybir.AxisListType
+
+STAGE1_BANK = BF16
+
+P = 128
+PACK = 4
+TOK = 512
+ROWS = TOK // P
+NCH = 8192 // TOK
+NGRP = 4
+DEPTH = 4
+
+
+def tile_channel_net_pa_kernel(tc, x, noise, h, W1, b1, W2, b2, out):
+    nc = tc.nc
+    x_v = x.rearrange("(p c r) k -> c p (r k)", c=NCH, r=ROWS)
+    n_v = noise.rearrange("(p g q) n -> g p (q n)", g=NGRP, q=ROWS * NCH // NGRP)
+    o_v = out.rearrange("(p c r) n -> c p (r n)", c=NCH, r=ROWS)
+
+    with ExitStack() as ctx:
+        const = ctx.enter_context(tc.tile_pool(name="const", bufs=1))
+        const2 = ctx.enter_context(tc.tile_pool(name="const2", bufs=2))
+        xin = ctx.enter_context(tc.tile_pool(name="xin", bufs=2 * NCH))
+        nin = ctx.enter_context(tc.tile_pool(name="nin", bufs=NGRP))
+        work = ctx.enter_context(tc.tile_pool(name="work", bufs=3))
+        yout = ctx.enter_context(tc.tile_pool(name="yout", bufs=4))
+        psum = ctx.enter_context(tc.psum_pool(name="psum", bufs=8))
+        ctx.enter_context(tc.manual_schedule())
+
+        def load_halves(pool, src, tag):
+            halves = []
+            for b in range(2):
+                half = pool.tile([P, 2 * 512], BF16, name=tag, tag=tag)
+                nc.sync.dma_start(out=half[:], in_=src[:, b * 1024 : (b + 1) * 1024])
+                halves.append(half)
+            return halves
+
+        w1_raw = load_halves(const2, W1.rearrange("(m t) k -> m (t k)", t=PACK), "w1_raw")
+        w2_raw = const.tile([P, 512], BF16, name="w2_raw")
+        x_sb = []
+        n_sb = []
+        for c in range(NCH):
+            x_sb.append(load_halves(xin, x_v[c], "x_half"))
+            if c == 0:
+                nc.sync.dma_start(out=w2_raw[:], in_=W2)
+            if c % (NCH // NGRP) == NCH // NGRP - 1:
+                n_g = nin.tile([P, ROWS * NCH // NGRP * P], BF16, name="n_g", tag="n_g")
+                nc.sync.dma_start(out=n_g[:], in_=n_v[c // (NCH // NGRP)])
+                n_sb.append(n_g)
+
+        b1_sb = const.tile([P, PACK], BF16, name="b1_sb")
+        h_sb = const.tile([P, 2], BF16, name="h_sb")
+        b2_sb = const.tile([P, 1], BF16, name="b2_sb")
+        b2x_sb = const.tile([P, 1], BF16, name="b2x_sb")
+        b2_pairs = b2.rearrange("(j w) -> j w", w=2)
+        with nc.allow_non_contiguous_dma(reason="small vectors, one or four elements a partition"):
+            nc.scalar.dma_start(out=b1_sb[:], in_=b1.rearrange("(p t) -> p t", t=PACK))
+            nc.scalar.dma_start(out=h_sb[:], in_=h.partition_broadcast(P))
+            nc.scalar.dma_start(out=b2_sb[:], in_=b2.rearrange("(c o) -> c o", o=1))
+            nc.scalar.dma_start(out=b2x_sb[0:P:2, :], in_=b2_pairs[:, 1:2])
+            nc.scalar.dma_start(out=b2x_sb[1:P:2, :], in_=b2_pairs[:, 0:1])
+
+        ident = const.tile([P, P], F32, name="ident")
+        make_identity(nc, ident[:])
+        warm_in = const.tile([P, 1], F32, name="warm_in")
+        warm_out = const.tile([P, 1], F32, name="warm_out")
+        nc.gpsimd.memset(warm_in[:], 1.0)
+        nc.scalar.activation(out=warm_out[:], in_=warm_in[:], func=ACT.Abs_reciprocal_sqrt)
+
+        def turn(tiles):
+            banks = []
+            for rows in tiles:
+                words = rows[:].bitcast(F32)
+                bank = psum.tile([P, 512], F32, name="turned", tag="bank")
+                for w in range(words.shape[1] // P):
+                    first = 256 * (w // 2)
+                    nc.tensor.transpose(
+                        bank[:, w * P : (w + 1) * P], words[:, first + w % 2 : first + 256 : 2], ident[:]
+                    )
+                banks.append(bank)
+            return banks
+
+        def lay(copy, grouped, b, bank):
+            copy(
+                out=grouped[:].bitcast(F32)[:, 512 * b : 512 * (b + 1)].rearrange("p (r i u) -> p r i u", r=2, u=2),
+                in_=bank[:].rearrange("p (r u i) -> p r i u", r=2, u=2),
+            )
+
+        w1_banks = turn(w1_raw)
+        w1_g = const.tile([P, PACK * 512], BF16, name="w1_g", align_bytes=64)
+        lay(nc.scalar.copy, w1_g, 0, w1_banks[0])
+        lay(nc.vector.tensor_copy, w1_g, 1, w1_banks[1])
+        w1_q = const.tile([P, 512], U32, name="w1_q", align_bytes=64)
+        w1_s = const.tile([P, 512], U8, name="w1_s", align_bytes=64)
+        nc.vector.quantize_mx(out=w1_q[:].bitcast(FP8X4), scales=w1_s[:], in_=w1_g[:])
+
+        w2_q = const.tile([P, 2 * P], U32, name="w2_q", align_bytes=64)
+        w2_s = const.tile([P, 2 * P], U8, name="w2_s", align_bytes=64)
+        h_f = const.tile([P, 2], F32, name="h_f")
+        tap_x = const.tile([P, 1], F32, name="tap_x")
+        bias_v = const.tile([P, 1], F32, name="bias_v")
+        inv_c = const.tile([P, 1], F32, name="inv_c")
+
+        def prepare_w2():
+            bank = live["w2t"]
+            w2_g = const.tile([P, 2 * 512], BF16, name="w2_g", align_bytes=64)
+            words = w2_g[:].bitcast(F32)
+            src = bank[:, 0:256]
+            nc.vector.tensor_copy(
+                out=words[:, 0:256].rearrange("p (c u) -> p c u", u=2), in_=src.rearrange("p (u c) -> p c u", u=2)
+            )
+            for w in range(2):
+                nc.vector.tensor_copy(
+                    out=words[:, 256:512].rearrange("p (j w u) -> p j w u", w=2, u=2)[:, :, w, :],
+                    in_=src.rearrange("p (u j w) -> p j w u", u=2, w=2)[:, :, 1 - w, :],
+                )
+            nc.vector.quantize_mx(out=w2_q[:].bitcast(FP8X4), scales=w2_s[:], in_=w2_g[:])
+
+        def prepare_constants():
+            odd = const.tile([P, 1], F32, name="odd")
+            sign = const.tile([P, 1], F32, name="sign")
+            part = const.tile([P, 1], F32, name="part")
+            h_sq = const.tile([P, 2], F32, name="h_sq")
+            h_n2 = const.tile([P, 1], F32, name="h_n2")
+            h_64 = const.tile([P, 1], F32, name="h_64")
+            nc.vector.tensor_copy(out=h_f[:], in_=h_sb[:])
+            nc.vector.tensor_reduce(out=odd[:], in_=ident[:, 1:P:2], axis=AX.X, op=ALU.add)
+            nc.vector.tensor_scalar(out=sign[:], in0=odd[:], scalar1=2.0, scalar2=-1.0, op0=ALU.mult, op1=ALU.add)
+            nc.vector.tensor_tensor(out=tap_x[:], in0=sign[:], in1=h_f[:, 1:2], op=ALU.mult)
+            nc.vector.tensor_tensor(out=part[:], in0=b2x_sb[:], in1=tap_x[:], op=ALU.mult)
+            nc.vector.scalar_tensor_tensor(
+                out=bias_v[:], in0=b2_sb[:], scalar=h_f[:, 0:1], in1=part[:], op0=ALU.mult, op1=ALU.add
+            )
+            nc.vector.tensor_tensor(out=h_sq[:], in0=h_f[:], in1=h_f[:], op=ALU.mult)
+            nc.vector.tensor_reduce(out=h_n2[:], in_=h_sq[:], axis=AX.X, op=ALU.add)
+            nc.vector.tensor_scalar(out=h_64[:], in0=h_n2[:], scalar1=64.0, scalar2=0.0, op0=ALU.mult, op1=ALU.add)
+            nc.vector.reciprocal(out=inv_c[:], in_=h_64[:])
+
+        live = {}
+
+        def x_turn(c):
+            live["xt", c] = turn(x_sb[c])
+
+        def x_lay(c):
+            x_g = work.tile([P, PACK * TOK], BF16, name="x_g", tag="x_g", align_bytes=64)
+            for b in range(2):
+                lay(nc.scalar.copy, x_g, b, live["xt", c][b])
+            live["xg", c] = x_g
+
+        def x_quant(c):
+            x_q = work.tile([P, TOK], U32, name="x_q", tag="x_q", align_bytes=64)
+            x_s = work.tile([P, TOK], U8, name="x_s", tag="x_s", align_bytes=64)
+            nc.vector.quantize_mx(out=x_q[:].bitcast(FP8X4), scales=x_s[:], in_=live["xg", c][:])
+            live["xq", c] = (x_q, x_s)
+
+        def stage1(c):
+            x_q, x_s = live["xq", c]
+            banks = []
+            for t in range(PACK):
+                bank = psum.tile([P, TOK], STAGE1_BANK, name="sum1", tag="bank")
+                nc.tensor.matmul_mx(
+                    out=bank[:],
+                    lhsT=w1_q[:, t * P : (t + 1) * P].bitcast(FP8X4),
+                    lhsT_scale=w1_s[:, t * P : (t + 1) * P],
+                    rhs=x_q[:].bitcast(FP8X4),
+                    rhs_scale=x_s[:],
+                    start=True,
+                    stop=True,
+                )
+                banks.append(bank)
+            live["s1", c] = banks
+            live["a", c] = work.tile([P, PACK, TOK], BF16, name="a_rows", tag="a_rows")
+
+        def read1_scalar(c, t):
+            nc.scalar.activation(
+                out=live["a", c][:, t, :], in_=live["s1", c][t][:], func=ACT.Relu, bias=b1_sb[:, t : t + 1], scale=1.0
+            )
+
+        def read1_vector(c, t):
+            nc.vector.tensor_scalar(
+                out=live["a", c][:, t, :],
+                in0=live["s1", c][t][:],
+                scalar1=b1_sb[:, t : t + 1],
+                scalar2=0.0,
+                op0=ALU.add,
+                op1=ALU.max,
+            )
+
+        def a_lay(c):
+            a_g = work.tile([P, PACK * TOK], BF16, name="a_g", tag="a_g", align_bytes=64)
+            nc.vector.tensor_copy(
+                out=a_g[:].rearrange("p (i t) -> p i t", t=PACK), in_=live["a", c][:].rearrange("p t i -> p i t")
+            )
+            live["ag", c] = a_g
+
+        def a_quant(c):
+            a_q = work.tile([P, TOK], U32, name="a_q", tag="a_q", align_bytes=64)
+            a_s = work.tile([P, TOK], U8, name="a_s", tag="a_s", align_bytes=64)
+            nc.vector.quantize_mx(out=a_q[:].bitcast(FP8X4), scales=a_s[:], in_=live["ag", c][:])
+            live["aq", c] = (a_q, a_s)
+
+        def stage2(c):
+            a_q, a_s = live["aq", c]
+            banks = []
+            for v in (1, 0):
+                bank = psum.tile([P, TOK], F32, name="sum2", tag="bank")
+                nc.tensor.matmul_mx(
+                    out=bank[:],
+                    lhsT=w2_q[:, v * P : (v + 1) * P].bitcast(FP8X4),
+                    lhsT_scale=w2_s[:, v * P : (v + 1) * P],
+                    rhs=a_q[:].bitcast(FP8X4),
+                    rhs_scale=a_s[:],
+                    start=True,
+                    stop=True,
+                )
+                banks.append(bank)
+            live["z", c] = banks
+
+        def tap_cross(c):
+            cross = work.tile([P, TOK], F32, name="cross", tag="cross")
+            nc.scalar.activation(
+                out=cross[:], in_=live["z", c][0][:], func=ACT.Identity, bias=bias_v[:, 0:1], scale=tap_x[:, 0:1]
+            )
+            live["cross", c] = cross
+
+        def tap_sum(c):
+            v_t = work.tile([P, TOK], F32, name="v_t", tag="v_t")
+            nc.vector.scalar_tensor_tensor(
+                out=v_t[:], in0=live["z", c][1][:], scalar=h_f[:, 0:1], in1=live["cross", c][:], op0=ALU.mult, op1=ALU.add
+            )
+            live["vt", c] = v_t
+
+        def v_turn(c):
+            bank = psum.tile([P, TOK], F32, name="v_rows", tag="bank")
+            for r in range(ROWS):
+                nc.tensor.transpose(bank[:, r * P : (r + 1) * P], live["vt", c][:, r * P : (r + 1) * P], ident[:])
+            live["v", c] = bank
+
+        def norms(c):
+            sq_sum = work.tile([P, ROWS], F32, name="sq_sum", tag="sq_sum")
+            for r in range(ROWS):
+                squares = work.tile([P, P], BF16, name="squares", tag="squares")
+                nc.scalar.activation(
+                    out=squares[:], in_=live["v", c][:, r * P : (r + 1) * P], func=ACT.Square, accum_out=sq_sum[:, r : r + 1]
+                )
+            gain = work.tile([P, ROWS], F32, name="gain", tag="gain")
+            nc.scalar.activation(out=gain[:], in_=sq_sum[:], func=ACT.Abs_reciprocal_sqrt, scale=inv_c[:, 0:1])
+            live["gain", c] = gain
+
+        def finish(c):
+            y = yout.tile([P, TOK], F32, name="y", tag="y")
+            per = NCH // NGRP
+            for r in range(ROWS):
+                first = ((c % per) * ROWS + r) * P
+                nc.vector.scalar_tensor_tensor(
+                    out=y[:, r * P : (r + 1) * P],
+                    in0=live["v", c][:, r * P : (r + 1) * P],
+                    scalar=live["gain", c][:, r : r + 1],
+                    in1=n_sb[c // per][:, first : first + P],
+                    op0=ALU.mult,
+                    op1=ALU.add,
+                )
+            nc.sync.dma_start(out=o_v[c], in_=y[:])
+
+        def on(c):
+            return 0 <= c < NCH
+
+        for i in range(NCH + DEPTH):
+            if on(i - 4):
+                v_turn(i - 4)
+            if on(i):
+                x_turn(i)
+            if i == 0:
+                live["w2t"] = turn([w2_raw])[0]
+            if on(i - 4):
+                norms(i - 4)
+            if on(i):
+                x_lay(i)
+            if on(i - 2):
+                a_lay(i - 2)
+            if on(i - 3):
+                tap_sum(i - 3)
+            if on(i - 2):
+                a_quant(i - 2)
+            if on(i - 1):
+                stage1(i - 1)
+                for t in range(PACK - 1):
+                    read1_scalar(i - 1, t)
+                read1_vector(i - 1, PACK - 1)
+            if on(i - 2):
+                stage2(i - 2)
+                tap_cross(i - 2)
+            if on(i - 4):
+                finish(i - 4)
+            if on(i):
+                x_quant(i)
+            if i == 0:
+                prepare_w2()
+                prepare_constants()

@@ -22,7 +22,8 @@ TOK = 512
 ROWS = TOK // P
 NCH = 8192 // TOK
 NGRP = 4
-DEPTH = 4
+VECTOR_BANKS = (1, 2)
+DEPTH = 5
 
 
 def tile_channel_net_pa_kernel(tc, x, noise, h, W1, b1, W2, b2, out):
@@ -203,7 +204,8 @@ def tile_channel_net_pa_kernel(tc, x, noise, h, W1, b1, W2, b2, out):
         def a_lay(c):
             a_g = work.tile([P, PACK * TOK], BF16, name="a_g", tag="a_g", align_bytes=64)
             nc.vector.tensor_copy(
-                out=a_g[:].rearrange("p (i t) -> p i t", t=PACK), in_=live["a", c][:].rearrange("p t i -> p i t")
+                out=a_g[:].rearrange("p (c i t) -> p c t i", i=4, t=PACK),
+                in_=live["a", c][:].rearrange("p t (c i) -> p c t i", i=4),
             )
             live["ag", c] = a_g
 
@@ -280,32 +282,34 @@ def tile_channel_net_pa_kernel(tc, x, noise, h, W1, b1, W2, b2, out):
             return 0 <= c < NCH
 
         for i in range(NCH + DEPTH):
-            if on(i - 4):
-                v_turn(i - 4)
+            if on(i - 5):
+                v_turn(i - 5)
             if on(i):
                 x_turn(i)
             if i == 0:
                 live["w2t"] = turn([w2_raw])[0]
-            if on(i - 4):
-                norms(i - 4)
+            if on(i - 5):
+                norms(i - 5)
             if on(i):
                 x_lay(i)
             if on(i - 2):
                 a_lay(i - 2)
-            if on(i - 3):
-                tap_sum(i - 3)
+            if on(i - 4):
+                tap_sum(i - 4)
             if on(i - 2):
                 a_quant(i - 2)
             if on(i - 1):
                 stage1(i - 1)
-                for t in range(PACK - 1):
+                by_vector = VECTOR_BANKS[(i - 1) % len(VECTOR_BANKS)]
+                for t in range(PACK - by_vector):
                     read1_scalar(i - 1, t)
-                read1_vector(i - 1, PACK - 1)
-            if on(i - 2):
-                stage2(i - 2)
-                tap_cross(i - 2)
-            if on(i - 4):
-                finish(i - 4)
+                for t in range(PACK - by_vector, PACK):
+                    read1_vector(i - 1, t)
+            if on(i - 3):
+                stage2(i - 3)
+                tap_cross(i - 3)
+            if on(i - 5):
+                finish(i - 5)
             if on(i):
                 x_quant(i)
             if i == 0:

@@ -22,7 +22,7 @@ TOK = 512
 ROWS = TOK // P
 NCH = 8192 // TOK
 NGRP = 4
-VECTOR_BANKS = (1, 2)
+VECTOR_BANKS = (2, 2)
 DEPTH = 5
 
 
@@ -66,14 +66,10 @@ def tile_channel_net_pa_kernel(tc, x, noise, h, W1, b1, W2, b2, out):
         b1_sb = const.tile([P, PACK], BF16, name="b1_sb")
         h_sb = const.tile([P, 2], BF16, name="h_sb")
         b2_sb = const.tile([P, 1], BF16, name="b2_sb")
-        b2x_sb = const.tile([P, 1], BF16, name="b2x_sb")
-        b2_pairs = b2.rearrange("(j w) -> j w", w=2)
         with nc.allow_non_contiguous_dma(reason="small vectors, one or four elements a partition"):
             nc.scalar.dma_start(out=b1_sb[:], in_=b1.rearrange("(p t) -> p t", t=PACK))
             nc.scalar.dma_start(out=h_sb[:], in_=h.partition_broadcast(P))
             nc.scalar.dma_start(out=b2_sb[:], in_=b2.rearrange("(c o) -> c o", o=1))
-            nc.scalar.dma_start(out=b2x_sb[0:P:2, :], in_=b2_pairs[:, 1:2])
-            nc.scalar.dma_start(out=b2x_sb[1:P:2, :], in_=b2_pairs[:, 0:1])
 
         ident = const.tile([P, P], F32, name="ident")
         make_identity(nc, ident[:])
@@ -109,42 +105,37 @@ def tile_channel_net_pa_kernel(tc, x, noise, h, W1, b1, W2, b2, out):
         w1_s = const.tile([P, 512], U8, name="w1_s", align_bytes=64)
         nc.vector.quantize_mx(out=w1_q[:].bitcast(FP8X4), scales=w1_s[:], in_=w1_g[:])
 
-        w2_q = const.tile([P, 2 * P], U32, name="w2_q", align_bytes=64)
-        w2_s = const.tile([P, 2 * P], U8, name="w2_s", align_bytes=64)
+        w2_q = const.tile([P, P], U32, name="w2_q", align_bytes=64)
+        w2_s = const.tile([P, P], U8, name="w2_s", align_bytes=64)
         h_f = const.tile([P, 2], F32, name="h_f")
-        tap_x = const.tile([P, 1], F32, name="tap_x")
-        bias_v = const.tile([P, 1], F32, name="bias_v")
+        tap = const.tile([P, P], F32, name="tap")
         inv_c = const.tile([P, 1], F32, name="inv_c")
 
         def prepare_w2():
             bank = live["w2t"]
-            w2_g = const.tile([P, 2 * 512], BF16, name="w2_g", align_bytes=64)
-            words = w2_g[:].bitcast(F32)
-            src = bank[:, 0:256]
+            w2_g = const.tile([P, 512], BF16, name="w2_g", align_bytes=64)
             nc.vector.tensor_copy(
-                out=words[:, 0:256].rearrange("p (c u) -> p c u", u=2), in_=src.rearrange("p (u c) -> p c u", u=2)
+                out=w2_g[:].bitcast(F32).rearrange("p (c u) -> p c u", u=2),
+                in_=bank[:, 0:256].rearrange("p (u c) -> p c u", u=2),
             )
-            for w in range(2):
-                nc.vector.tensor_copy(
-                    out=words[:, 256:512].rearrange("p (j w u) -> p j w u", w=2, u=2)[:, :, w, :],
-                    in_=src.rearrange("p (u j w) -> p j w u", u=2, w=2)[:, :, 1 - w, :],
-                )
             nc.vector.quantize_mx(out=w2_q[:].bitcast(FP8X4), scales=w2_s[:], in_=w2_g[:])
 
         def prepare_constants():
-            odd = const.tile([P, 1], F32, name="odd")
-            sign = const.tile([P, 1], F32, name="sign")
-            part = const.tile([P, 1], F32, name="part")
+            swap = const.tile([P, P], F32, name="swap")
             h_sq = const.tile([P, 2], F32, name="h_sq")
             h_n2 = const.tile([P, 1], F32, name="h_n2")
             h_64 = const.tile([P, 1], F32, name="h_64")
             nc.vector.tensor_copy(out=h_f[:], in_=h_sb[:])
-            nc.vector.tensor_reduce(out=odd[:], in_=ident[:, 1:P:2], axis=AX.X, op=ALU.add)
-            nc.vector.tensor_scalar(out=sign[:], in0=odd[:], scalar1=2.0, scalar2=-1.0, op0=ALU.mult, op1=ALU.add)
-            nc.vector.tensor_tensor(out=tap_x[:], in0=sign[:], in1=h_f[:, 1:2], op=ALU.mult)
-            nc.vector.tensor_tensor(out=part[:], in0=b2x_sb[:], in1=tap_x[:], op=ALU.mult)
+            id_pairs = ident[:].rearrange("p (j w) -> p j w", w=2)
+            swap_pairs = swap[:].rearrange("p (j w) -> p j w", w=2)
+            nc.vector.tensor_scalar(
+                out=swap_pairs[:, :, 0], in0=id_pairs[:, :, 1], scalar1=h_f[:, 1:2], scalar2=-1.0, op0=ALU.mult, op1=ALU.mult
+            )
+            nc.vector.tensor_scalar(
+                out=swap_pairs[:, :, 1], in0=id_pairs[:, :, 0], scalar1=h_f[:, 1:2], scalar2=1.0, op0=ALU.mult, op1=ALU.mult
+            )
             nc.vector.scalar_tensor_tensor(
-                out=bias_v[:], in0=b2_sb[:], scalar=h_f[:, 0:1], in1=part[:], op0=ALU.mult, op1=ALU.add
+                out=tap[:], in0=ident[:], scalar=h_f[:, 0:1], in1=swap[:], op0=ALU.mult, op1=ALU.add
             )
             nc.vector.tensor_tensor(out=h_sq[:], in0=h_f[:], in1=h_f[:], op=ALU.mult)
             nc.vector.tensor_reduce(out=h_n2[:], in_=h_sq[:], axis=AX.X, op=ALU.add)
@@ -217,39 +208,29 @@ def tile_channel_net_pa_kernel(tc, x, noise, h, W1, b1, W2, b2, out):
 
         def stage2(c):
             a_q, a_s = live["aq", c]
-            banks = []
-            for v in (1, 0):
-                bank = psum.tile([P, TOK], F32, name="sum2", tag="bank")
-                nc.tensor.matmul_mx(
-                    out=bank[:],
-                    lhsT=w2_q[:, v * P : (v + 1) * P].bitcast(FP8X4),
-                    lhsT_scale=w2_s[:, v * P : (v + 1) * P],
-                    rhs=a_q[:].bitcast(FP8X4),
-                    rhs_scale=a_s[:],
-                    start=True,
-                    stop=True,
-                )
-                banks.append(bank)
-            live["z", c] = banks
-
-        def tap_cross(c):
-            cross = work.tile([P, TOK], F32, name="cross", tag="cross")
-            nc.scalar.activation(
-                out=cross[:], in_=live["z", c][0][:], func=ACT.Identity, bias=bias_v[:, 0:1], scale=tap_x[:, 0:1]
+            bank = psum.tile([P, TOK], F32, name="sum2", tag="bank")
+            nc.tensor.matmul_mx(
+                out=bank[:],
+                lhsT=w2_q[:].bitcast(FP8X4),
+                lhsT_scale=w2_s[:],
+                rhs=a_q[:].bitcast(FP8X4),
+                rhs_scale=a_s[:],
+                start=True,
+                stop=True,
             )
-            live["cross", c] = cross
+            live["z", c] = bank
 
-        def tap_sum(c):
-            v_t = work.tile([P, TOK], F32, name="v_t", tag="v_t")
-            nc.vector.scalar_tensor_tensor(
-                out=v_t[:], in0=live["z", c][1][:], scalar=h_f[:, 0:1], in1=live["cross", c][:], op0=ALU.mult, op1=ALU.add
-            )
-            live["vt", c] = v_t
+        def u_read(c):
+            u_t = work.tile([P, TOK], F32, name="u_t", tag="u_t")
+            nc.scalar.activation(out=u_t[:], in_=live["z", c][:], func=ACT.Identity, bias=b2_sb[:, 0:1], scale=1.0)
+            live["u", c] = u_t
 
-        def v_turn(c):
+        def rotate(c):
             bank = psum.tile([P, TOK], F32, name="v_rows", tag="bank")
             for r in range(ROWS):
-                nc.tensor.transpose(bank[:, r * P : (r + 1) * P], live["vt", c][:, r * P : (r + 1) * P], ident[:])
+                nc.tensor.matmul(
+                    out=bank[:, r * P : (r + 1) * P], lhsT=live["u", c][:, r * P : (r + 1) * P], rhs=tap[:], start=True, stop=True
+                )
             live["v", c] = bank
 
         def norms(c):
@@ -282,22 +263,16 @@ def tile_channel_net_pa_kernel(tc, x, noise, h, W1, b1, W2, b2, out):
             return 0 <= c < NCH
 
         for i in range(NCH + DEPTH):
-            if on(i - 5):
-                v_turn(i - 5)
             if on(i):
                 x_turn(i)
             if i == 0:
                 live["w2t"] = turn([w2_raw])[0]
-            if on(i - 5):
-                norms(i - 5)
             if on(i):
                 x_lay(i)
+            if on(i - 5):
+                finish(i - 5)
             if on(i - 2):
                 a_lay(i - 2)
-            if on(i - 4):
-                tap_sum(i - 4)
-            if on(i - 2):
-                a_quant(i - 2)
             if on(i - 1):
                 stage1(i - 1)
                 by_vector = VECTOR_BANKS[(i - 1) % len(VECTOR_BANKS)]
@@ -305,11 +280,14 @@ def tile_channel_net_pa_kernel(tc, x, noise, h, W1, b1, W2, b2, out):
                     read1_scalar(i - 1, t)
                 for t in range(PACK - by_vector, PACK):
                     read1_vector(i - 1, t)
+            if on(i - 2):
+                a_quant(i - 2)
             if on(i - 3):
                 stage2(i - 3)
-                tap_cross(i - 3)
-            if on(i - 5):
-                finish(i - 5)
+                u_read(i - 3)
+            if on(i - 4):
+                rotate(i - 4)
+                norms(i - 4)
             if on(i):
                 x_quant(i)
             if i == 0:

@@ -272,7 +272,7 @@ def tile_channel_net_pa_kernel(tc, x, noise, h, W1, b1, W2, b2, out):
             if on(i - 5):
                 finish(i - 5)
             if on(i - 2):
-                a_lay(i - 2)
+                a_quant(i - 2)
             if on(i - 1):
                 stage1(i - 1)
                 by_vector = VECTOR_BANKS[(i - 1) % len(VECTOR_BANKS)]
@@ -280,16 +280,16 @@ def tile_channel_net_pa_kernel(tc, x, noise, h, W1, b1, W2, b2, out):
                     read1_scalar(i - 1, t)
                 for t in range(PACK - by_vector, PACK):
                     read1_vector(i - 1, t)
-            if on(i - 2):
-                a_quant(i - 2)
+            if on(i):
+                x_quant(i)
+            if i == 0:
+                prepare_w2()
+                prepare_constants()
+            if on(i - 1):
+                a_lay(i - 1)
             if on(i - 3):
                 stage2(i - 3)
                 u_read(i - 3)
             if on(i - 4):
                 rotate(i - 4)
                 norms(i - 4)
-            if on(i):
-                x_quant(i)
-            if i == 0:
-                prepare_w2()
-                prepare_constants()

@@ -269,8 +269,10 @@ def tile_channel_net_pa_kernel(tc, x, noise, h, W1, b1, W2, b2, out):
                 live["w2t"] = turn([w2_raw])[0]
             if on(i):
                 x_lay(i)
-            if on(i - 5):
-                finish(i - 5)
+                x_quant(i)
+            if i == 0:
+                prepare_w2()
+                prepare_constants()
             if on(i - 2):
                 a_quant(i - 2)
             if on(i - 1):
@@ -280,11 +282,8 @@ def tile_channel_net_pa_kernel(tc, x, noise, h, W1, b1, W2, b2, out):
                     read1_scalar(i - 1, t)
                 for t in range(PACK - by_vector, PACK):
                     read1_vector(i - 1, t)
-            if on(i):
-                x_quant(i)
-            if i == 0:
-                prepare_w2()
-                prepare_constants()
+            if on(i - 5):
+                finish(i - 5)
             if on(i - 1):
                 a_lay(i - 1)
             if on(i - 3):

@@ -12,15 +12,15 @@ U8 = mybir.dt.uint8
 FP8X4 = mybir.dt.float8_e4m3fn_x4
 ACT = mybir.ActivationFunctionType
 ALU = mybir.AluOpType
-AX = mybir.AxisListType
 
 STAGE1_BANK = BF16
 
 P = 128
 PACK = 4
-TOK = 512
-ROWS = TOK // P
-NCH = 8192 // TOK
+NROWS = 8192 // P
+CHUNK_ROWS = (1, 1, 2) + (4,) * 14 + (2, 1, 1)
+NCH = len(CHUNK_ROWS)
+FIRST_ROW = tuple(sum(CHUNK_ROWS[:c]) for c in range(NCH))
 NGRP = 4
 VECTOR_BANKS = (2, 2)
 DEPTH = 5
@@ -28,39 +28,38 @@ DEPTH = 5
 
 def tile_channel_net_pa_kernel(tc, x, noise, h, W1, b1, W2, b2, out):
     nc = tc.nc
-    x_v = x.rearrange("(p c r) k -> c p (r k)", c=NCH, r=ROWS)
-    n_v = noise.rearrange("(p g q) n -> g p (q n)", g=NGRP, q=ROWS * NCH // NGRP)
-    o_v = out.rearrange("(p c r) n -> c p (r n)", c=NCH, r=ROWS)
+    x_v = x.rearrange("(p j r) k -> j p (r k)", j=NROWS // 2, r=2)
+    n_v = noise.rearrange("(p g q) n -> g p (q n)", g=NGRP, q=NROWS // NGRP)
+    o_v = out.rearrange("(p q) n -> p (q n)", q=NROWS)
 
     with ExitStack() as ctx:
         const = ctx.enter_context(tc.tile_pool(name="const", bufs=1))
         const2 = ctx.enter_context(tc.tile_pool(name="const2", bufs=2))
-        xin = ctx.enter_context(tc.tile_pool(name="xin", bufs=2 * NCH))
+        xin = ctx.enter_context(tc.tile_pool(name="xin", bufs=NROWS // 2))
         nin = ctx.enter_context(tc.tile_pool(name="nin", bufs=NGRP))
         work = ctx.enter_context(tc.tile_pool(name="work", bufs=3))
         yout = ctx.enter_context(tc.tile_pool(name="yout", bufs=4))
         psum = ctx.enter_context(tc.psum_pool(name="psum", bufs=8))
         ctx.enter_context(tc.manual_schedule())
 
-        def load_halves(pool, src, tag):
-            halves = []
-            for b in range(2):
-                half = pool.tile([P, 2 * 512], BF16, name=tag, tag=tag)
-                nc.sync.dma_start(out=half[:], in_=src[:, b * 1024 : (b + 1) * 1024])
-                halves.append(half)
-            return halves
+        def load_pair(pool, src, tag):
+            pair = pool.tile([P, 2 * 512], BF16, name=tag, tag=tag)
+            nc.sync.dma_start(out=pair[:], in_=src)
+            return pair
 
-        w1_raw = load_halves(const2, W1.rearrange("(m t) k -> m (t k)", t=PACK), "w1_raw")
+        w1_v = W1.rearrange("(m t) k -> m (t k)", t=PACK)
+        w1_raw = [load_pair(const2, w1_v[:, b * 1024 : (b + 1) * 1024], "w1_raw") for b in range(2)]
         w2_raw = const.tile([P, 512], BF16, name="w2_raw")
         x_sb = []
         n_sb = []
-        for c in range(NCH):
-            x_sb.append(load_halves(xin, x_v[c], "x_half"))
-            if c == 0:
+        per = NROWS // 2 // NGRP
+        for j in range(NROWS // 2):
+            x_sb.append(load_pair(xin, x_v[j], "x_pair"))
+            if j == 1:
                 nc.sync.dma_start(out=w2_raw[:], in_=W2)
-            if c % (NCH // NGRP) == NCH // NGRP - 1:
-                n_g = nin.tile([P, ROWS * NCH // NGRP * P], BF16, name="n_g", tag="n_g")
-                nc.sync.dma_start(out=n_g[:], in_=n_v[c // (NCH // NGRP)])
+            if j % per == per - 1:
+                n_g = nin.tile([P, NROWS // NGRP * P], BF16, name="n_g", tag="n_g")
+                nc.sync.dma_start(out=n_g[:], in_=n_v[j // per])
                 n_sb.append(n_g)
 
         b1_sb = const.tile([P, PACK], BF16, name="b1_sb")
@@ -78,29 +77,26 @@ def tile_channel_net_pa_kernel(tc, x, noise, h, W1, b1, W2, b2, out):
         nc.gpsimd.memset(warm_in[:], 1.0)
         nc.scalar.activation(out=warm_out[:], in_=warm_in[:], func=ACT.Abs_reciprocal_sqrt)
 
-        def turn(tiles):
-            banks = []
-            for rows in tiles:
-                words = rows[:].bitcast(F32)
-                bank = psum.tile([P, 512], F32, name="turned", tag="bank")
-                for w in range(words.shape[1] // P):
-                    first = 256 * (w // 2)
+        def turn(rows):
+            bank = psum.tile([P, 512], F32, name="turned", tag="bank")
+            for r, (tile_, k) in enumerate(rows):
+                words = tile_[:].bitcast(F32)
+                for u in range(2):
                     nc.tensor.transpose(
-                        bank[:, w * P : (w + 1) * P], words[:, first + w % 2 : first + 256 : 2], ident[:]
+                        bank[:, (2 * r + u) * P : (2 * r + u + 1) * P], words[:, 256 * k + u : 256 * (k + 1) : 2], ident[:]
                     )
-                banks.append(bank)
-            return banks
+            return bank
 
-        def lay(copy, grouped, b, bank):
+        def lay(copy, grouped, first, n, bank):
             copy(
-                out=grouped[:].bitcast(F32)[:, 512 * b : 512 * (b + 1)].rearrange("p (r i u) -> p r i u", r=2, u=2),
-                in_=bank[:].rearrange("p (r u i) -> p r i u", r=2, u=2),
+                out=grouped[:].bitcast(F32)[:, 256 * first : 256 * (first + n)].rearrange("p (r i u) -> p r i u", r=n, u=2),
+                in_=bank[:, 0 : 256 * n].rearrange("p (r u i) -> p r i u", r=n, u=2),
             )
 
-        w1_banks = turn(w1_raw)
+        w1_banks = [turn([(w1_raw[b], 0), (w1_raw[b], 1)]) for b in range(2)]
         w1_g = const.tile([P, PACK * 512], BF16, name="w1_g", align_bytes=64)
-        lay(nc.scalar.copy, w1_g, 0, w1_banks[0])
-        lay(nc.vector.tensor_copy, w1_g, 1, w1_banks[1])
+        lay(nc.scalar.copy, w1_g, 0, 2, w1_banks[0])
+        lay(nc.vector.tensor_copy, w1_g, 2, 2, w1_banks[1])
         w1_q = const.tile([P, 512], U32, name="w1_q", align_bytes=64)
         w1_s = const.tile([P, 512], U8, name="w1_s", align_bytes=64)
         nc.vector.quantize_mx(out=w1_q[:].bitcast(FP8X4), scales=w1_s[:], in_=w1_g[:])
@@ -111,51 +107,59 @@ def tile_channel_net_pa_kernel(tc, x, noise, h, W1, b1, W2, b2, out):
         tap = const.tile([P, P], F32, name="tap")
         inv_c = const.tile([P, 1], F32, name="inv_c")
 
-        def prepare_w2():
-            bank = live["w2t"]
-            w2_g = const.tile([P, 512], BF16, name="w2_g", align_bytes=64)
-            nc.vector.tensor_copy(
-                out=w2_g[:].bitcast(F32).rearrange("p (c u) -> p c u", u=2),
-                in_=bank[:, 0:256].rearrange("p (u c) -> p c u", u=2),
-            )
-            nc.vector.quantize_mx(out=w2_q[:].bitcast(FP8X4), scales=w2_s[:], in_=w2_g[:])
+        w2_g = const.tile([P, 512], BF16, name="w2_g", align_bytes=64)
 
-        def prepare_constants():
-            swap = const.tile([P, P], F32, name="swap")
-            h_sq = const.tile([P, 2], F32, name="h_sq")
-            h_n2 = const.tile([P, 1], F32, name="h_n2")
-            h_64 = const.tile([P, 1], F32, name="h_64")
-            nc.vector.tensor_copy(out=h_f[:], in_=h_sb[:])
-            id_pairs = ident[:].rearrange("p (j w) -> p j w", w=2)
-            swap_pairs = swap[:].rearrange("p (j w) -> p j w", w=2)
-            nc.vector.tensor_scalar(
-                out=swap_pairs[:, :, 0], in0=id_pairs[:, :, 1], scalar1=h_f[:, 1:2], scalar2=-1.0, op0=ALU.mult, op1=ALU.mult
+        def lay_w2():
+            nc.scalar.copy(
+                out=w2_g[:].bitcast(F32).rearrange("p (c u) -> p c u", u=2),
+                in_=live["w2t"][:, 0:256].rearrange("p (u c) -> p c u", u=2),
             )
-            nc.vector.tensor_scalar(
-                out=swap_pairs[:, :, 1], in0=id_pairs[:, :, 0], scalar1=h_f[:, 1:2], scalar2=1.0, op0=ALU.mult, op1=ALU.mult
-            )
-            nc.vector.scalar_tensor_tensor(
-                out=tap[:], in0=ident[:], scalar=h_f[:, 0:1], in1=swap[:], op0=ALU.mult, op1=ALU.add
-            )
-            nc.vector.tensor_tensor(out=h_sq[:], in0=h_f[:], in1=h_f[:], op=ALU.mult)
-            nc.vector.tensor_reduce(out=h_n2[:], in_=h_sq[:], axis=AX.X, op=ALU.add)
-            nc.vector.tensor_scalar(out=h_64[:], in0=h_n2[:], scalar1=64.0, scalar2=0.0, op0=ALU.mult, op1=ALU.add)
+
+        def quantize_w2():
+            nc.vector.quantize_mx(out=w2_q[:].bitcast(FP8X4), scales=w2_s[:], in_=w2_g[:])
             nc.vector.reciprocal(out=inv_c[:], in_=h_64[:])
+
+        swap = const.tile([P, P], F32, name="swap")
+        diag = const.tile([P, P], F32, name="diag")
+        h_sq = const.tile([P, 2], F32, name="h_sq")
+        h_n2 = const.tile([P, 1], F32, name="h_n2")
+        h_64 = const.tile([P, 1], F32, name="h_64")
+        nc.gpsimd.tensor_copy(out=h_f[:], in_=h_sb[:])
+        id_pairs = ident[:].rearrange("p (j w) -> p j w", w=2)
+        swap_pairs = swap[:].rearrange("p (j w) -> p j w", w=2)
+        nc.gpsimd.tensor_scalar(
+            out=swap_pairs[:, :, 0], in0=id_pairs[:, :, 1], scalar1=h_f[:, 1:2], scalar2=-1.0, op0=ALU.mult, op1=ALU.mult
+        )
+        nc.gpsimd.tensor_scalar(
+            out=swap_pairs[:, :, 1], in0=id_pairs[:, :, 0], scalar1=h_f[:, 1:2], scalar2=1.0, op0=ALU.mult, op1=ALU.mult
+        )
+        nc.gpsimd.tensor_scalar(out=diag[:], in0=ident[:], scalar1=h_f[:, 0:1], scalar2=1.0, op0=ALU.mult, op1=ALU.mult)
+        nc.gpsimd.tensor_tensor(out=tap[:], in0=diag[:], in1=swap[:], op=ALU.add)
+        nc.gpsimd.tensor_tensor(out=h_sq[:], in0=h_f[:], in1=h_f[:], op=ALU.mult)
+        nc.gpsimd.tensor_tensor(out=h_n2[:], in0=h_sq[:, 0:1], in1=h_sq[:, 1:2], op=ALU.add)
+        nc.gpsimd.tensor_scalar(out=h_64[:], in0=h_n2[:], scalar1=64.0, scalar2=1.0, op0=ALU.mult, op1=ALU.mult)
 
         live = {}
 
+        def tokens(c):
+            return CHUNK_ROWS[c] * P
+
         def x_turn(c):
-            live["xt", c] = turn(x_sb[c])
+            banks = []
+            for b in range(0, CHUNK_ROWS[c], 2):
+                qs = [FIRST_ROW[c] + b + k for k in range(min(2, CHUNK_ROWS[c] - b))]
+                banks.append((b, len(qs), turn([(x_sb[q // 2], q % 2) for q in qs])))
+            live["xt", c] = banks
 
         def x_lay(c):
-            x_g = work.tile([P, PACK * TOK], BF16, name="x_g", tag="x_g", align_bytes=64)
-            for b in range(2):
-                lay(nc.scalar.copy, x_g, b, live["xt", c][b])
+            x_g = work.tile([P, PACK * tokens(c)], BF16, name="x_g", tag="x_g", align_bytes=64)
+            for first, n, bank in live["xt", c]:
+                lay(nc.scalar.copy, x_g, first, n, bank)
             live["xg", c] = x_g
 
         def x_quant(c):
-            x_q = work.tile([P, TOK], U32, name="x_q", tag="x_q", align_bytes=64)
-            x_s = work.tile([P, TOK], U8, name="x_s", tag="x_s", align_bytes=64)
+            x_q = work.tile([P, tokens(c)], U32, name="x_q", tag="x_q", align_bytes=64)
+            x_s = work.tile([P, tokens(c)], U8, name="x_s", tag="x_s", align_bytes=64)
             nc.vector.quantize_mx(out=x_q[:].bitcast(FP8X4), scales=x_s[:], in_=live["xg", c][:])
             live["xq", c] = (x_q, x_s)
 
@@ -163,7 +167,7 @@ def tile_channel_net_pa_kernel(tc, x, noise, h, W1, b1, W2, b2, out):
             x_q, x_s = live["xq", c]
             banks = []
             for t in range(PACK):
-                bank = psum.tile([P, TOK], STAGE1_BANK, name="sum1", tag="bank")
+                bank = psum.tile([P, tokens(c)], STAGE1_BANK, name="sum1", tag="bank")
                 nc.tensor.matmul_mx(
                     out=bank[:],
                     lhsT=w1_q[:, t * P : (t + 1) * P].bitcast(FP8X4),
@@ -175,7 +179,7 @@ def tile_channel_net_pa_kernel(tc, x, noise, h, W1, b1, W2, b2, out):
                 )
                 banks.append(bank)
             live["s1", c] = banks
-            live["a", c] = work.tile([P, PACK, TOK], BF16, name="a_rows", tag="a_rows")
+            live["a", c] = work.tile([P, PACK, tokens(c)], BF16, name="a_rows", tag="a_rows")
 
         def read1_scalar(c, t):
             nc.scalar.activation(
@@ -193,7 +197,7 @@ def tile_channel_net_pa_kernel(tc, x, noise, h, W1, b1, W2, b2, out):
             )
 
         def a_lay(c):
-            a_g = work.tile([P, PACK * TOK], BF16, name="a_g", tag="a_g", align_bytes=64)
+            a_g = work.tile([P, PACK * tokens(c)], BF16, name="a_g", tag="a_g", align_bytes=64)
             nc.vector.tensor_copy(
                 out=a_g[:].rearrange("p (c i t) -> p c t i", i=4, t=PACK),
                 in_=live["a", c][:].rearrange("p t (c i) -> p c t i", i=4),
@@ -201,14 +205,14 @@ def tile_channel_net_pa_kernel(tc, x, noise, h, W1, b1, W2, b2, out):
             live["ag", c] = a_g
 
         def a_quant(c):
-            a_q = work.tile([P, TOK], U32, name="a_q", tag="a_q", align_bytes=64)
-            a_s = work.tile([P, TOK], U8, name="a_s", tag="a_s", align_bytes=64)
+            a_q = work.tile([P, tokens(c)], U32, name="a_q", tag="a_q", align_bytes=64)
+            a_s = work.tile([P, tokens(c)], U8, name="a_s", tag="a_s", align_bytes=64)
             nc.vector.quantize_mx(out=a_q[:].bitcast(FP8X4), scales=a_s[:], in_=live["ag", c][:])
             live["aq", c] = (a_q, a_s)
 
         def stage2(c):
             a_q, a_s = live["aq", c]
-            bank = psum.tile([P, TOK], F32, name="sum2", tag="bank")
+            bank = psum.tile([P, tokens(c)], F32, name="sum2", tag="bank")
             nc.tensor.matmul_mx(
                 out=bank[:],
                 lhsT=w2_q[:].bitcast(FP8X4),
@@ -221,43 +225,43 @@ def tile_channel_net_pa_kernel(tc, x, noise, h, W1, b1, W2, b2, out):
             live["z", c] = bank
 
         def u_read(c):
-            u_t = work.tile([P, TOK], F32, name="u_t", tag="u_t")
+            u_t = work.tile([P, tokens(c)], F32, name="u_t", tag="u_t")
             nc.scalar.activation(out=u_t[:], in_=live["z", c][:], func=ACT.Identity, bias=b2_sb[:, 0:1], scale=1.0)
             live["u", c] = u_t
 
         def rotate(c):
-            bank = psum.tile([P, TOK], F32, name="v_rows", tag="bank")
-            for r in range(ROWS):
+            bank = psum.tile([P, tokens(c)], F32, name="v_rows", tag="bank")
+            for r in range(CHUNK_ROWS[c]):
                 nc.tensor.matmul(
                     out=bank[:, r * P : (r + 1) * P], lhsT=live["u", c][:, r * P : (r + 1) * P], rhs=tap[:], start=True, stop=True
                 )
             live["v", c] = bank
 
         def norms(c):
-            sq_sum = work.tile([P, ROWS], F32, name="sq_sum", tag="sq_sum")
-            for r in range(ROWS):
+            sq_sum = work.tile([P, CHUNK_ROWS[c]], F32, name="sq_sum", tag="sq_sum")
+            for r in range(CHUNK_ROWS[c]):
                 squares = work.tile([P, P], BF16, name="squares", tag="squares")
                 nc.scalar.activation(
                     out=squares[:], in_=live["v", c][:, r * P : (r + 1) * P], func=ACT.Square, accum_out=sq_sum[:, r : r + 1]
                 )
-            gain = work.tile([P, ROWS], F32, name="gain", tag="gain")
+            gain = work.tile([P, CHUNK_ROWS[c]], F32, name="gain", tag="gain")
             nc.scalar.activation(out=gain[:], in_=sq_sum[:], func=ACT.Abs_reciprocal_sqrt, scale=inv_c[:, 0:1])
             live["gain", c] = gain
 
         def finish(c):
-            y = yout.tile([P, TOK], F32, name="y", tag="y")
-            per = NCH // NGRP
-            for r in range(ROWS):
-                first = ((c % per) * ROWS + r) * P
+            y = yout.tile([P, tokens(c)], F32, name="y", tag="y")
+            for r in range(CHUNK_ROWS[c]):
+                q = FIRST_ROW[c] + r
+                first = q % (NROWS // NGRP) * P
                 nc.vector.scalar_tensor_tensor(
                     out=y[:, r * P : (r + 1) * P],
                     in0=live["v", c][:, r * P : (r + 1) * P],
                     scalar=live["gain", c][:, r : r + 1],
-                    in1=n_sb[c // per][:, first : first + P],
+                    in1=n_sb[q // (NROWS // NGRP)][:, first : first + P],
                     op0=ALU.mult,
                     op1=ALU.add,
                 )
-            nc.sync.dma_start(out=o_v[c], in_=y[:])
+            nc.sync.dma_start(out=o_v[:, FIRST_ROW[c] * P : (FIRST_ROW[c] + CHUNK_ROWS[c]) * P], in_=y[:])
 
         def on(c):
             return 0 <= c < NCH
@@ -266,13 +270,14 @@ def tile_channel_net_pa_kernel(tc, x, noise, h, W1, b1, W2, b2, out):
             if on(i):
                 x_turn(i)
             if i == 0:
-                live["w2t"] = turn([w2_raw])[0]
+                live["w2t"] = turn([(w2_raw, 0)])
             if on(i):
                 x_lay(i)
                 x_quant(i)
             if i == 0:
-                prepare_w2()
-                prepare_constants()
+                lay_w2()
+            if i == 1:
+                quantize_w2()
             if on(i - 2):
                 a_quant(i - 2)
             if on(i - 1):

@@ -167,9 +167,10 @@ def tile_channel_net_pa_kernel(tc, x, noise, h, W1, b1, W2, b2, out):
             x_q, x_s = live["xq", c]
             banks = []
             for t in range(PACK):
-                bank = psum.tile([P, tokens(c)], STAGE1_BANK, name="sum1", tag="bank")
+                if t % 2 == 0:
+                    banks.append(psum.tile([P, 2, tokens(c)], STAGE1_BANK, name="sum1", tag="bank"))
                 nc.tensor.matmul_mx(
-                    out=bank[:],
+                    out=banks[t // 2][:, t % 2, :],
                     lhsT=w1_q[:, t * P : (t + 1) * P].bitcast(FP8X4),
                     lhsT_scale=w1_s[:, t * P : (t + 1) * P],
                     rhs=x_q[:].bitcast(FP8X4),
@@ -177,19 +178,18 @@ def tile_channel_net_pa_kernel(tc, x, noise, h, W1, b1, W2, b2, out):
                     start=True,
                     stop=True,
                 )
-                banks.append(bank)
             live["s1", c] = banks
             live["a", c] = work.tile([P, PACK, tokens(c)], BF16, name="a_rows", tag="a_rows")
 
         def read1_scalar(c, t):
             nc.scalar.activation(
-                out=live["a", c][:, t, :], in_=live["s1", c][t][:], func=ACT.Relu, bias=b1_sb[:, t : t + 1], scale=1.0
+                out=live["a", c][:, t, :], in_=live["s1", c][t // 2][:, t % 2, :], func=ACT.Relu, bias=b1_sb[:, t : t + 1], scale=1.0
             )
 
         def read1_vector(c, t):
             nc.vector.tensor_scalar(
                 out=live["a", c][:, t, :],
-                in0=live["s1", c][t][:],
+                in0=live["s1", c][t // 2][:, t % 2, :],
                 scalar1=b1_sb[:, t : t + 1],
                 scalar2=0.0,
                 op0=ALU.add,

@@ -22,7 +22,6 @@ CHUNK_ROWS = (1, 1, 2) + (4,) * 14 + (2, 1, 1)
 NCH = len(CHUNK_ROWS)
 FIRST_ROW = tuple(sum(CHUNK_ROWS[:c]) for c in range(NCH))
 NGRP = 4
-VECTOR_BANKS = (2, 2)
 DEPTH = 5
 
 
@@ -91,6 +90,14 @@ def tile_channel_net_pa_kernel(tc, x, noise, h, W1, b1, W2, b2, out):
             copy(
                 out=grouped[:].bitcast(F32)[:, 256 * first : 256 * (first + n)].rearrange("p (r i u) -> p r i u", r=n, u=2),
                 in_=bank[:, 0 : 256 * n].rearrange("p (r u i) -> p r i u", r=n, u=2),
+            )
+
+        zeros = const.tile([P, 512], BF16, name="zeros")
+        b1_wide = const.tile([P, 2, 512], BF16, name="b1_wide")
+        nc.vector.memset(zeros[:], 0.0)
+        for t in range(2):
+            nc.vector.tensor_scalar(
+                out=b1_wide[:, t, :], in0=zeros[:], scalar1=b1_sb[:, 2 + t : 3 + t], scalar2=0.0, op0=ALU.add, op1=ALU.add
             )
 
         w1_banks = [turn([(w1_raw[b], 0), (w1_raw[b], 1)]) for b in range(2)]
@@ -186,21 +193,17 @@ def tile_channel_net_pa_kernel(tc, x, noise, h, W1, b1, W2, b2, out):
                 out=live["a", c][:, t, :], in_=live["s1", c][t // 2][:, t % 2, :], func=ACT.Relu, bias=b1_sb[:, t : t + 1], scale=1.0
             )
 
-        def read1_vector(c, t):
-            nc.vector.tensor_scalar(
-                out=live["a", c][:, t, :],
-                in0=live["s1", c][t // 2][:, t % 2, :],
-                scalar1=b1_sb[:, t : t + 1],
-                scalar2=0.0,
-                op0=ALU.add,
-                op1=ALU.max,
+        def read1_vector_pair(c):
+            nc.vector.tensor_tensor(
+                out=live["a", c][:, 2:4, :], in0=live["s1", c][1][:], in1=b1_wide[:, :, 0 : tokens(c)], op=ALU.add
             )
 
         def a_lay(c):
             a_g = work.tile([P, PACK * tokens(c)], BF16, name="a_g", tag="a_g", align_bytes=64)
-            nc.vector.tensor_copy(
+            nc.vector.tensor_scalar_max(
                 out=a_g[:].rearrange("p (c i t) -> p c t i", i=4, t=PACK),
-                in_=live["a", c][:].rearrange("p t (c i) -> p c t i", i=4),
+                in0=live["a", c][:].rearrange("p t (c i) -> p c t i", i=4),
+                scalar1=0.0,
             )
             live["ag", c] = a_g
 
@@ -282,11 +285,9 @@ def tile_channel_net_pa_kernel(tc, x, noise, h, W1, b1, W2, b2, out):
                 a_quant(i - 2)
             if on(i - 1):
                 stage1(i - 1)
-                by_vector = VECTOR_BANKS[(i - 1) % len(VECTOR_BANKS)]
-                for t in range(PACK - by_vector):
+                for t in range(2):
                     read1_scalar(i - 1, t)
-                for t in range(PACK - by_vector, PACK):
-                    read1_vector(i - 1, t)
+                read1_vector_pair(i - 1)
             if on(i - 5):
                 finish(i - 5)
             if on(i - 1):

@@ -270,9 +270,8 @@ def tile_channel_net_pa_kernel(tc, x, noise, h, W1, b1, W2, b2, out):
             return 0 <= c < NCH
 
         for i in range(NCH + DEPTH):
-            if on(i):
-                x_turn(i)
             if i == 0:
+                x_turn(0)
                 live["w2t"] = turn([(w2_raw, 0)])
             if on(i):
                 x_lay(i)
@@ -297,4 +296,9 @@ def tile_channel_net_pa_kernel(tc, x, noise, h, W1, b1, W2, b2, out):
                 u_read(i - 3)
             if on(i - 4):
                 rotate(i - 4)
+            if i % 2 == 0:
+                for c in (i + 1, i + 2):
+                    if on(c):
+                        x_turn(c)
+            if on(i - 4):
                 norms(i - 4)

@@ -19,6 +19,11 @@ P = 128
 PACK = 4
 NROWS = 8192 // P
 CHUNK_ROWS = (1, 1, 2) + (4,) * 14 + (2, 1, 1)
+LEAD = 0
+TURN_EACH = False
+DEFER_GAIN = True
+W2_LATE = False
+VK3_EVERY = 0
 NCH = len(CHUNK_ROWS)
 FIRST_ROW = tuple(sum(CHUNK_ROWS[:c]) for c in range(NCH))
 NGRP = 4
@@ -54,7 +59,7 @@ def tile_channel_net_pa_kernel(tc, x, noise, h, W1, b1, W2, b2, out):
         per = NROWS // 2 // NGRP
         for j in range(NROWS // 2):
             x_sb.append(load_pair(xin, x_v[j], "x_pair"))
-            if j == 1:
+            if j == (3 if W2_LATE else 1):
                 nc.sync.dma_start(out=w2_raw[:], in_=W2)
             if j % per == per - 1:
                 n_g = nin.tile([P, NROWS // NGRP * P], BF16, name="n_g", tag="n_g")
@@ -165,8 +170,8 @@ def tile_channel_net_pa_kernel(tc, x, noise, h, W1, b1, W2, b2, out):
             live["xg", c] = x_g
 
         def x_quant(c):
-            x_q = work.tile([P, tokens(c)], U32, name="x_q", tag="x_q", align_bytes=64)
-            x_s = work.tile([P, tokens(c)], U8, name="x_s", tag="x_s", align_bytes=64)
+            x_q = work.tile([P, tokens(c)], U32, name="x_q", tag="x_q", align_bytes=64, bufs=3 + LEAD)
+            x_s = work.tile([P, tokens(c)], U8, name="x_s", tag="x_s", align_bytes=64, bufs=3 + LEAD)
             nc.vector.quantize_mx(out=x_q[:].bitcast(FP8X4), scales=x_s[:], in_=live["xg", c][:])
             live["xq", c] = (x_q, x_s)
 
@@ -191,6 +196,15 @@ def tile_channel_net_pa_kernel(tc, x, noise, h, W1, b1, W2, b2, out):
         def read1_scalar(c, t):
             nc.scalar.activation(
                 out=live["a", c][:, t, :], in_=live["s1", c][t // 2][:, t % 2, :], func=ACT.Relu, bias=b1_sb[:, t : t + 1], scale=1.0
+            )
+
+        def vector_pieces(c):
+            return 3 if (VK3_EVERY and CHUNK_ROWS[c] == 4 and c % VK3_EVERY == VK3_EVERY - 1) else 2
+
+        def read1_vector_one(c, t):
+            nc.vector.tensor_scalar(
+                out=live["a", c][:, t, :], in0=live["s1", c][t // 2][:, t % 2, :], scalar1=b1_sb[:, t : t + 1], scalar2=0.0,
+                op0=ALU.add, op1=ALU.max,
             )
 
         def read1_vector_pair(c):
@@ -247,8 +261,13 @@ def tile_channel_net_pa_kernel(tc, x, noise, h, W1, b1, W2, b2, out):
                 nc.scalar.activation(
                     out=squares[:], in_=live["v", c][:, r * P : (r + 1) * P], func=ACT.Square, accum_out=sq_sum[:, r : r + 1]
                 )
+            live["sq", c] = sq_sum
+            if not DEFER_GAIN:
+                gain_of(c)
+
+        def gain_of(c):
             gain = work.tile([P, CHUNK_ROWS[c]], F32, name="gain", tag="gain")
-            nc.scalar.activation(out=gain[:], in_=sq_sum[:], func=ACT.Abs_reciprocal_sqrt, scale=inv_c[:, 0:1])
+            nc.scalar.activation(out=gain[:], in_=live["sq", c][:], func=ACT.Abs_reciprocal_sqrt, scale=inv_c[:, 0:1])
             live["gain", c] = gain
 
         def finish(c):
@@ -269,23 +288,30 @@ def tile_channel_net_pa_kernel(tc, x, noise, h, W1, b1, W2, b2, out):
         def on(c):
             return 0 <= c < NCH
 
-        for i in range(NCH + DEPTH):
-            if i == 0:
+        for i in range(-LEAD, NCH + DEPTH):
+            j = i + LEAD
+            first_round = i == -LEAD
+            if first_round:
                 x_turn(0)
-                live["w2t"] = turn([(w2_raw, 0)])
-            if on(i):
-                x_lay(i)
-                x_quant(i)
-            if i == 0:
+                if not W2_LATE:
+                    live["w2t"] = turn([(w2_raw, 0)])
+            if on(j):
+                x_lay(j)
+                x_quant(j)
+            if DEFER_GAIN and on(i - 5):
+                gain_of(i - 5)
+            if i == -LEAD + (2 if W2_LATE else 0):
                 lay_w2()
-            if i == 1:
+            if i == -LEAD + (2 if W2_LATE else 1):
                 quantize_w2()
             if on(i - 2):
                 a_quant(i - 2)
             if on(i - 1):
                 stage1(i - 1)
-                for t in range(2):
+                for t in range(4 - vector_pieces(i - 1)):
                     read1_scalar(i - 1, t)
+                if vector_pieces(i - 1) == 3:
+                    read1_vector_one(i - 1, 1)
                 read1_vector_pair(i - 1)
             if on(i - 5):
                 finish(i - 5)
@@ -296,9 +322,14 @@ def tile_channel_net_pa_kernel(tc, x, noise, h, W1, b1, W2, b2, out):
                 u_read(i - 3)
             if on(i - 4):
                 rotate(i - 4)
-            if i % 2 == 0:
-                for c in (i + 1, i + 2):
+            if TURN_EACH:
+                if on(j + 1):
+                    x_turn(j + 1)
+            elif j % 2 == 0:
+                for c in (j + 1, j + 2):
                     if on(c):
                         x_turn(c)
+            if W2_LATE and i == -LEAD + 1:
+                live["w2t"] = turn([(w2_raw, 0)])
             if on(i - 4):
                 norms(i - 4)

@@ -18,11 +18,13 @@ STAGE1_BANK = BF16
 P = 128
 PACK = 4
 NROWS = 8192 // P
-CHUNK_ROWS = (1, 1, 2) + (4,) * 14 + (2, 1, 1)
+CHUNK_ROWS = (2,) + (4,) * 15 + (1, 1)
 LEAD = 0
-TURN_EACH = False
+TURN_EACH = True
 DEFER_GAIN = True
 W2_LATE = False
+PAIR_FIRST = True
+FINISH_LAST = False
 VK3_EVERY = 0
 NCH = len(CHUNK_ROWS)
 FIRST_ROW = tuple(sum(CHUNK_ROWS[:c]) for c in range(NCH))
@@ -288,48 +290,58 @@ def tile_channel_net_pa_kernel(tc, x, noise, h, W1, b1, W2, b2, out):
         def on(c):
             return 0 <= c < NCH
 
-        for i in range(-LEAD, NCH + DEPTH):
-            j = i + LEAD
-            first_round = i == -LEAD
-            if first_round:
+        for i in range(NCH + DEPTH):
+            gain_due = on(i - 5)
+            if i == 0:
                 x_turn(0)
-                if not W2_LATE:
-                    live["w2t"] = turn([(w2_raw, 0)])
-            if on(j):
-                x_lay(j)
-                x_quant(j)
-            if DEFER_GAIN and on(i - 5):
-                gain_of(i - 5)
-            if i == -LEAD + (2 if W2_LATE else 0):
+                live["w2t"] = turn([(w2_raw, 0)])
+            if on(i):
+                x_lay(i)
+                x_quant(i)
+                if gain_due:
+                    gain_of(i - 5)
+                    gain_due = False
+            if i == 0:
                 lay_w2()
-            if i == -LEAD + (2 if W2_LATE else 1):
+            if i == 1:
                 quantize_w2()
-            if on(i - 2):
+            if not PAIR_FIRST and on(i - 2):
                 a_quant(i - 2)
             if on(i - 1):
                 stage1(i - 1)
                 for t in range(4 - vector_pieces(i - 1)):
                     read1_scalar(i - 1, t)
+                if gain_due:
+                    gain_of(i - 5)
+                    gain_due = False
                 if vector_pieces(i - 1) == 3:
                     read1_vector_one(i - 1, 1)
                 read1_vector_pair(i - 1)
+            if PAIR_FIRST and on(i - 2):
+                a_quant(i - 2)
+            early_u = gain_due and on(i - 3)
+            if early_u:
+                stage2(i - 3)
+                u_read(i - 3)
+            if gain_due:
+                gain_of(i - 5)
+            if FINISH_LAST and on(i - 1):
+                a_lay(i - 1)
             if on(i - 5):
                 finish(i - 5)
-            if on(i - 1):
+            if not FINISH_LAST and on(i - 1):
                 a_lay(i - 1)
-            if on(i - 3):
+            if on(i - 3) and not early_u:
                 stage2(i - 3)
                 u_read(i - 3)
             if on(i - 4):
                 rotate(i - 4)
             if TURN_EACH:
-                if on(j + 1):
-                    x_turn(j + 1)
-            elif j % 2 == 0:
-                for c in (j + 1, j + 2):
+                if on(i + 1):
+                    x_turn(i + 1)
+            elif i % 2 == 0:
+                for c in (i + 1, i + 2):
                     if on(c):
                         x_turn(c)
-            if W2_LATE and i == -LEAD + 1:
-                live["w2t"] = turn([(w2_raw, 0)])
             if on(i - 4):
                 norms(i - 4)

@@ -25,6 +25,10 @@ DEFER_GAIN = True
 W2_LATE = False
 PAIR_FIRST = True
 FINISH_LAST = False
+WARM = (3, 1, 1, 1)
+HYBRID = False
+VK1_EVERY = 0
+XLAY_REVERSED = False
 VK3_EVERY = 0
 NCH = len(CHUNK_ROWS)
 FIRST_ROW = tuple(sum(CHUNK_ROWS[:c]) for c in range(NCH))
@@ -107,7 +111,15 @@ def tile_channel_net_pa_kernel(tc, x, noise, h, W1, b1, W2, b2, out):
                 out=b1_wide[:, t, :], in0=zeros[:], scalar1=b1_sb[:, 2 + t : 3 + t], scalar2=0.0, op0=ALU.add, op1=ALU.add
             )
 
+        warm_bank = psum.tile([P, 512], F32, name="warm_bank", tag="bank") if sum(WARM) else None
+
+        def keep_warm(n):
+            for k in range(n):
+                nc.tensor.matmul(out=warm_bank[:], lhsT=zeros[:, 0:P], rhs=zeros[:], start=True, stop=True)
+
+        keep_warm(WARM[0])
         w1_banks = [turn([(w1_raw[b], 0), (w1_raw[b], 1)]) for b in range(2)]
+        keep_warm(WARM[1])
         w1_g = const.tile([P, PACK * 512], BF16, name="w1_g", align_bytes=64)
         lay(nc.scalar.copy, w1_g, 0, 2, w1_banks[0])
         lay(nc.vector.tensor_copy, w1_g, 2, 2, w1_banks[1])
@@ -167,7 +179,7 @@ def tile_channel_net_pa_kernel(tc, x, noise, h, W1, b1, W2, b2, out):
 
         def x_lay(c):
             x_g = work.tile([P, PACK * tokens(c)], BF16, name="x_g", tag="x_g", align_bytes=64)
-            for first, n, bank in live["xt", c]:
+            for first, n, bank in (reversed(live["xt", c]) if XLAY_REVERSED else live["xt", c]):
                 lay(nc.scalar.copy, x_g, first, n, bank)
             live["xg", c] = x_g
 
@@ -201,6 +213,8 @@ def tile_channel_net_pa_kernel(tc, x, noise, h, W1, b1, W2, b2, out):
             )
 
         def vector_pieces(c):
+            if VK1_EVERY and CHUNK_ROWS[c] == 4 and c % VK1_EVERY == VK1_EVERY - 1:
+                return 1
             return 3 if (VK3_EVERY and CHUNK_ROWS[c] == 4 and c % VK3_EVERY == VK3_EVERY - 1) else 2
 
         def read1_vector_one(c, t):
@@ -292,9 +306,12 @@ def tile_channel_net_pa_kernel(tc, x, noise, h, W1, b1, W2, b2, out):
 
         for i in range(NCH + DEPTH):
             gain_due = on(i - 5)
+            pair_first = PAIR_FIRST and not (HYBRID and on(i) and on(i - 5))
             if i == 0:
                 x_turn(0)
+                keep_warm(WARM[2])
                 live["w2t"] = turn([(w2_raw, 0)])
+                keep_warm(WARM[3])
             if on(i):
                 x_lay(i)
                 x_quant(i)
@@ -305,7 +322,7 @@ def tile_channel_net_pa_kernel(tc, x, noise, h, W1, b1, W2, b2, out):
                 lay_w2()
             if i == 1:
                 quantize_w2()
-            if not PAIR_FIRST and on(i - 2):
+            if not pair_first and on(i - 2):
                 a_quant(i - 2)
             if on(i - 1):
                 stage1(i - 1)
@@ -316,8 +333,11 @@ def tile_channel_net_pa_kernel(tc, x, noise, h, W1, b1, W2, b2, out):
                     gain_due = False
                 if vector_pieces(i - 1) == 3:
                     read1_vector_one(i - 1, 1)
-                read1_vector_pair(i - 1)
-            if PAIR_FIRST and on(i - 2):
+                if vector_pieces(i - 1) == 1:
+                    read1_vector_one(i - 1, 3)
+                else:
+                    read1_vector_pair(i - 1)
+            if pair_first and on(i - 2):
                 a_quant(i - 2)
             early_u = gain_due and on(i - 3)
             if early_u:

@@ -25,9 +25,14 @@ DEFER_GAIN = True
 W2_LATE = False
 PAIR_FIRST = True
 FINISH_LAST = False
+RUN = 8
+DMA_LAID = ()
+W1_QUARTERS = False
+W2_BEHIND = False
 WARM = (3, 1, 1, 1)
 HYBRID = False
 VK1_EVERY = 0
+VK1_CHUNKS = ()
 XLAY_REVERSED = False
 VK3_EVERY = 0
 NCH = len(CHUNK_ROWS)
@@ -58,14 +63,41 @@ def tile_channel_net_pa_kernel(tc, x, noise, h, W1, b1, W2, b2, out):
             return pair
 
         w1_v = W1.rearrange("(m t) k -> m (t k)", t=PACK)
-        w1_raw = [load_pair(const2, w1_v[:, b * 1024 : (b + 1) * 1024], "w1_raw") for b in range(2)]
+        def load_halves(pool, src, tag):
+            pair = pool.tile([P, 2 * 512], BF16, name=tag, tag=tag)
+            for k in range(2):
+                nc.sync.dma_start(out=pair[:, k * 512 : (k + 1) * 512], in_=src[:, k * 512 : (k + 1) * 512])
+            return pair
+
+        w1_load = load_halves if W1_QUARTERS else load_pair
+        w1_raw = [w1_load(const2, w1_v[:, b * 1024 : (b + 1) * 1024], "w1_raw") for b in range(2)]
         w2_raw = const.tile([P, 512], BF16, name="w2_raw")
         x_sb = []
         n_sb = []
         per = NROWS // 2 // NGRP
+        laid_rows = [FIRST_ROW[c] + r for c in DMA_LAID for r in range(CHUNK_ROWS[c])]
+        x_8 = x.rearrange("(i q) (p t) -> q p i t", q=NROWS, t=PACK)
+        laid = ctx.enter_context(tc.tile_pool(name="laid", bufs=1))
+
+        def lay_by_dma(c):
+            x_g = laid.tile([P, PACK * CHUNK_ROWS[c] * P], BF16, name="x_laid%d" % c, align_bytes=64)
+            with nc.allow_non_contiguous_dma(reason="four neighbouring k of a token, 8 bytes, to each partition"):
+                for r in range(CHUNK_ROWS[c]):
+                    nc.sync.dma_start(
+                        out=x_g[:, r * 512 : (r + 1) * 512].rearrange("p (i t) -> p i t", t=PACK), in_=x_8[FIRST_ROW[c] + r]
+                    )
+            live_laid[c] = x_g
+
+        live_laid = {}
         for j in range(NROWS // 2):
-            x_sb.append(load_pair(xin, x_v[j], "x_pair"))
-            if j == (3 if W2_LATE else 1):
+            if 2 * j in laid_rows and 2 * j + 1 in laid_rows:
+                x_sb.append(None)
+                for c in DMA_LAID:
+                    if FIRST_ROW[c] + CHUNK_ROWS[c] - 1 in (2 * j, 2 * j + 1):
+                        lay_by_dma(c)
+            else:
+                x_sb.append(load_pair(xin, x_v[j], "x_pair"))
+            if j == (2 if W2_BEHIND else 1):
                 nc.sync.dma_start(out=w2_raw[:], in_=W2)
             if j % per == per - 1:
                 n_g = nin.tile([P, NROWS // NGRP * P], BF16, name="n_g", tag="n_g")
@@ -171,6 +203,8 @@ def tile_channel_net_pa_kernel(tc, x, noise, h, W1, b1, W2, b2, out):
             return CHUNK_ROWS[c] * P
 
         def x_turn(c):
+            if c in DMA_LAID:
+                return
             banks = []
             for b in range(0, CHUNK_ROWS[c], 2):
                 qs = [FIRST_ROW[c] + b + k for k in range(min(2, CHUNK_ROWS[c] - b))]
@@ -178,6 +212,9 @@ def tile_channel_net_pa_kernel(tc, x, noise, h, W1, b1, W2, b2, out):
             live["xt", c] = banks
 
         def x_lay(c):
+            if c in DMA_LAID:
+                live["xg", c] = live_laid[c]
+                return
             x_g = work.tile([P, PACK * tokens(c)], BF16, name="x_g", tag="x_g", align_bytes=64)
             for first, n, bank in (reversed(live["xt", c]) if XLAY_REVERSED else live["xt", c]):
                 lay(nc.scalar.copy, x_g, first, n, bank)
@@ -215,6 +252,8 @@ def tile_channel_net_pa_kernel(tc, x, noise, h, W1, b1, W2, b2, out):
         def vector_pieces(c):
             if VK1_EVERY and CHUNK_ROWS[c] == 4 and c % VK1_EVERY == VK1_EVERY - 1:
                 return 1
+            if c in VK1_CHUNKS:
+                return 1
             return 3 if (VK3_EVERY and CHUNK_ROWS[c] == 4 and c % VK3_EVERY == VK3_EVERY - 1) else 2
 
         def read1_vector_one(c, t):
@@ -231,8 +270,8 @@ def tile_channel_net_pa_kernel(tc, x, noise, h, W1, b1, W2, b2, out):
         def a_lay(c):
             a_g = work.tile([P, PACK * tokens(c)], BF16, name="a_g", tag="a_g", align_bytes=64)
             nc.vector.tensor_scalar_max(
-                out=a_g[:].rearrange("p (c i t) -> p c t i", i=4, t=PACK),
-                in0=live["a", c][:].rearrange("p t (c i) -> p c t i", i=4),
+                out=a_g[:].rearrange("p (c i t) -> p c t i", i=RUN, t=PACK),
+                in0=live["a", c][:].rearrange("p t (c i) -> p c t i", i=RUN),
                 scalar1=0.0,
             )
             live["ag", c] = a_g
@@ -310,15 +349,16 @@ def tile_channel_net_pa_kernel(tc, x, noise, h, W1, b1, W2, b2, out):
             if i == 0:
                 x_turn(0)
                 keep_warm(WARM[2])
-                live["w2t"] = turn([(w2_raw, 0)])
-                keep_warm(WARM[3])
+                if not W2_BEHIND:
+                    live["w2t"] = turn([(w2_raw, 0)])
+                    keep_warm(WARM[3])
             if on(i):
                 x_lay(i)
                 x_quant(i)
                 if gain_due:
                     gain_of(i - 5)
                     gain_due = False
-            if i == 0:
+            if i == (1 if W2_BEHIND else 0):
                 lay_w2()
             if i == 1:
                 quantize_w2()
@@ -359,6 +399,9 @@ def tile_channel_net_pa_kernel(tc, x, noise, h, W1, b1, W2, b2, out):
             if TURN_EACH:
                 if on(i + 1):
                     x_turn(i + 1)
+                if W2_BEHIND and i == 0:
+                    live["w2t"] = turn([(w2_raw, 0)])
+                    keep_warm(WARM[3])
             elif i % 2 == 0:
                 for c in (i + 1, i + 2):
                     if on(c):

@@ -25,6 +25,7 @@ DEFER_GAIN = True
 W2_LATE = False
 PAIR_FIRST = True
 FINISH_LAST = False
+GAIN_BETWEEN = True
 RUN = 8
 DMA_LAID = ()
 W1_QUARTERS = False
@@ -211,13 +212,15 @@ def tile_channel_net_pa_kernel(tc, x, noise, h, W1, b1, W2, b2, out):
                 banks.append((b, len(qs), turn([(x_sb[q // 2], q % 2) for q in qs])))
             live["xt", c] = banks
 
-        def x_lay(c):
+        def x_lay(c, gain_chunk=None):
             if c in DMA_LAID:
                 live["xg", c] = live_laid[c]
                 return
             x_g = work.tile([P, PACK * tokens(c)], BF16, name="x_g", tag="x_g", align_bytes=64)
             for first, n, bank in (reversed(live["xt", c]) if XLAY_REVERSED else live["xt", c]):
                 lay(nc.scalar.copy, x_g, first, n, bank)
+                if gain_chunk is not None and first == 0:
+                    gain_of(gain_chunk)
             live["xg", c] = x_g
 
         def x_quant(c):
@@ -353,7 +356,11 @@ def tile_channel_net_pa_kernel(tc, x, noise, h, W1, b1, W2, b2, out):
                     live["w2t"] = turn([(w2_raw, 0)])
                     keep_warm(WARM[3])
             if on(i):
-                x_lay(i)
+                if GAIN_BETWEEN and gain_due:
+                    x_lay(i, i - 5)
+                    gain_due = False
+                else:
+                    x_lay(i)
                 x_quant(i)
                 if gain_due:
                     gain_of(i - 5)

from contextlib import ExitStack

import concourse.mybir as mybir
from concourse.masks import make_identity

FLOPS = 2 * 8192 * 512 * 512 + 2 * 8192 * 512 * 128

F32 = mybir.dt.float32
BF16 = mybir.dt.bfloat16
U32 = mybir.dt.uint32
U8 = mybir.dt.uint8
FP8X4 = mybir.dt.float8_e4m3fn_x4
ACT = mybir.ActivationFunctionType
ALU = mybir.AluOpType

STAGE1_BANK = BF16

P = 128
PACK = 4
NROWS = 8192 // P
CHUNK_ROWS = (2,) + (4,) * 15 + (1, 1)
LEAD = 0
TURN_EACH = True
DEFER_GAIN = True
W2_LATE = False
PAIR_FIRST = True
FINISH_LAST = False
GAIN_BETWEEN = True
RUN = 8
DMA_LAID = ()
W1_QUARTERS = False
W2_BEHIND = False
WARM = (3, 1, 1, 1)
HYBRID = False
VK1_EVERY = 0
VK1_CHUNKS = ()
XLAY_REVERSED = False
VK3_EVERY = 0
NCH = len(CHUNK_ROWS)
FIRST_ROW = tuple(sum(CHUNK_ROWS[:c]) for c in range(NCH))
NGRP = 4
DEPTH = 5


def tile_channel_net_pa_kernel(tc, x, noise, h, W1, b1, W2, b2, out):
    nc = tc.nc
    x_v = x.rearrange("(p j r) k -> j p (r k)", j=NROWS // 2, r=2)
    n_v = noise.rearrange("(p g q) n -> g p (q n)", g=NGRP, q=NROWS // NGRP)
    o_v = out.rearrange("(p q) n -> p (q n)", q=NROWS)

    with ExitStack() as ctx:
        const = ctx.enter_context(tc.tile_pool(name="const", bufs=1))
        const2 = ctx.enter_context(tc.tile_pool(name="const2", bufs=2))
        xin = ctx.enter_context(tc.tile_pool(name="xin", bufs=NROWS // 2))
        nin = ctx.enter_context(tc.tile_pool(name="nin", bufs=NGRP))
        work = ctx.enter_context(tc.tile_pool(name="work", bufs=3))
        yout = ctx.enter_context(tc.tile_pool(name="yout", bufs=4))
        psum = ctx.enter_context(tc.psum_pool(name="psum", bufs=8))
        ctx.enter_context(tc.manual_schedule())

        def load_pair(pool, src, tag):
            pair = pool.tile([P, 2 * 512], BF16, name=tag, tag=tag)
            nc.sync.dma_start(out=pair[:], in_=src)
            return pair

        w1_v = W1.rearrange("(m t) k -> m (t k)", t=PACK)
        def load_halves(pool, src, tag):
            pair = pool.tile([P, 2 * 512], BF16, name=tag, tag=tag)
            for k in range(2):
                nc.sync.dma_start(out=pair[:, k * 512 : (k + 1) * 512], in_=src[:, k * 512 : (k + 1) * 512])
            return pair

        w1_load = load_halves if W1_QUARTERS else load_pair
        w1_raw = [w1_load(const2, w1_v[:, b * 1024 : (b + 1) * 1024], "w1_raw") for b in range(2)]
        w2_raw = const.tile([P, 512], BF16, name="w2_raw")
        x_sb = []
        n_sb = []
        per = NROWS // 2 // NGRP
        laid_rows = [FIRST_ROW[c] + r for c in DMA_LAID for r in range(CHUNK_ROWS[c])]
        x_8 = x.rearrange("(i q) (p t) -> q p i t", q=NROWS, t=PACK)
        laid = ctx.enter_context(tc.tile_pool(name="laid", bufs=1))

        def lay_by_dma(c):
            x_g = laid.tile([P, PACK * CHUNK_ROWS[c] * P], BF16, name="x_laid%d" % c, align_bytes=64)
            with nc.allow_non_contiguous_dma(reason="four neighbouring k of a token, 8 bytes, to each partition"):
                for r in range(CHUNK_ROWS[c]):
                    nc.sync.dma_start(
                        out=x_g[:, r * 512 : (r + 1) * 512].rearrange("p (i t) -> p i t", t=PACK), in_=x_8[FIRST_ROW[c] + r]
                    )
            live_laid[c] = x_g

        live_laid = {}
        for j in range(NROWS // 2):
            if 2 * j in laid_rows and 2 * j + 1 in laid_rows:
                x_sb.append(None)
                for c in DMA_LAID:
                    if FIRST_ROW[c] + CHUNK_ROWS[c] - 1 in (2 * j, 2 * j + 1):
                        lay_by_dma(c)
            else:
                x_sb.append(load_pair(xin, x_v[j], "x_pair"))
            if j == (2 if W2_BEHIND else 1):
                nc.sync.dma_start(out=w2_raw[:], in_=W2)
            if j % per == per - 1:
                n_g = nin.tile([P, NROWS // NGRP * P], BF16, name="n_g", tag="n_g")
                nc.sync.dma_start(out=n_g[:], in_=n_v[j // per])
                n_sb.append(n_g)

        b1_sb = const.tile([P, PACK], BF16, name="b1_sb")
        h_sb = const.tile([P, 2], BF16, name="h_sb")
        b2_sb = const.tile([P, 1], BF16, name="b2_sb")
        with nc.allow_non_contiguous_dma(reason="small vectors, one or four elements a partition"):
            nc.scalar.dma_start(out=b1_sb[:], in_=b1.rearrange("(p t) -> p t", t=PACK))
            nc.scalar.dma_start(out=h_sb[:], in_=h.partition_broadcast(P))
            nc.scalar.dma_start(out=b2_sb[:], in_=b2.rearrange("(c o) -> c o", o=1))

        ident = const.tile([P, P], F32, name="ident")
        make_identity(nc, ident[:])
        warm_in = const.tile([P, 1], F32, name="warm_in")
        warm_out = const.tile([P, 1], F32, name="warm_out")
        nc.gpsimd.memset(warm_in[:], 1.0)
        nc.scalar.activation(out=warm_out[:], in_=warm_in[:], func=ACT.Abs_reciprocal_sqrt)

        def turn(rows):
            bank = psum.tile([P, 512], F32, name="turned", tag="bank")
            for r, (tile_, k) in enumerate(rows):
                words = tile_[:].bitcast(F32)
                for u in range(2):
                    nc.tensor.transpose(
                        bank[:, (2 * r + u) * P : (2 * r + u + 1) * P], words[:, 256 * k + u : 256 * (k + 1) : 2], ident[:]
                    )
            return bank

        def lay(copy, grouped, first, n, bank):
            copy(
                out=grouped[:].bitcast(F32)[:, 256 * first : 256 * (first + n)].rearrange("p (r i u) -> p r i u", r=n, u=2),
                in_=bank[:, 0 : 256 * n].rearrange("p (r u i) -> p r i u", r=n, u=2),
            )

        zeros = const.tile([P, 512], BF16, name="zeros")
        b1_wide = const.tile([P, 2, 512], BF16, name="b1_wide")
        nc.vector.memset(zeros[:], 0.0)
        for t in range(2):
            nc.vector.tensor_scalar(
                out=b1_wide[:, t, :], in0=zeros[:], scalar1=b1_sb[:, 2 + t : 3 + t], scalar2=0.0, op0=ALU.add, op1=ALU.add
            )

        warm_bank = psum.tile([P, 512], F32, name="warm_bank", tag="bank") if sum(WARM) else None

        def keep_warm(n):
            for k in range(n):
                nc.tensor.matmul(out=warm_bank[:], lhsT=zeros[:, 0:P], rhs=zeros[:], start=True, stop=True)

        keep_warm(WARM[0])
        w1_banks = [turn([(w1_raw[b], 0), (w1_raw[b], 1)]) for b in range(2)]
        keep_warm(WARM[1])
        w1_g = const.tile([P, PACK * 512], BF16, name="w1_g", align_bytes=64)
        lay(nc.scalar.copy, w1_g, 0, 2, w1_banks[0])
        lay(nc.vector.tensor_copy, w1_g, 2, 2, w1_banks[1])
        w1_q = const.tile([P, 512], U32, name="w1_q", align_bytes=64)
        w1_s = const.tile([P, 512], U8, name="w1_s", align_bytes=64)
        nc.vector.quantize_mx(out=w1_q[:].bitcast(FP8X4), scales=w1_s[:], in_=w1_g[:])

        w2_q = const.tile([P, P], U32, name="w2_q", align_bytes=64)
        w2_s = const.tile([P, P], U8, name="w2_s", align_bytes=64)
        h_f = const.tile([P, 2], F32, name="h_f")
        tap = const.tile([P, P], F32, name="tap")
        inv_c = const.tile([P, 1], F32, name="inv_c")

        w2_g = const.tile([P, 512], BF16, name="w2_g", align_bytes=64)

        def lay_w2():
            nc.scalar.copy(
                out=w2_g[:].bitcast(F32).rearrange("p (c u) -> p c u", u=2),
                in_=live["w2t"][:, 0:256].rearrange("p (u c) -> p c u", u=2),
            )

        def quantize_w2():
            nc.vector.quantize_mx(out=w2_q[:].bitcast(FP8X4), scales=w2_s[:], in_=w2_g[:])
            nc.vector.reciprocal(out=inv_c[:], in_=h_64[:])

        swap = const.tile([P, P], F32, name="swap")
        diag = const.tile([P, P], F32, name="diag")
        h_sq = const.tile([P, 2], F32, name="h_sq")
        h_n2 = const.tile([P, 1], F32, name="h_n2")
        h_64 = const.tile([P, 1], F32, name="h_64")
        nc.gpsimd.tensor_copy(out=h_f[:], in_=h_sb[:])
        id_pairs = ident[:].rearrange("p (j w) -> p j w", w=2)
        swap_pairs = swap[:].rearrange("p (j w) -> p j w", w=2)
        nc.gpsimd.tensor_scalar(
            out=swap_pairs[:, :, 0], in0=id_pairs[:, :, 1], scalar1=h_f[:, 1:2], scalar2=-1.0, op0=ALU.mult, op1=ALU.mult
        )
        nc.gpsimd.tensor_scalar(
            out=swap_pairs[:, :, 1], in0=id_pairs[:, :, 0], scalar1=h_f[:, 1:2], scalar2=1.0, op0=ALU.mult, op1=ALU.mult
        )
        nc.gpsimd.tensor_scalar(out=diag[:], in0=ident[:], scalar1=h_f[:, 0:1], scalar2=1.0, op0=ALU.mult, op1=ALU.mult)
        nc.gpsimd.tensor_tensor(out=tap[:], in0=diag[:], in1=swap[:], op=ALU.add)
        nc.gpsimd.tensor_tensor(out=h_sq[:], in0=h_f[:], in1=h_f[:], op=ALU.mult)
        nc.gpsimd.tensor_tensor(out=h_n2[:], in0=h_sq[:, 0:1], in1=h_sq[:, 1:2], op=ALU.add)
        nc.gpsimd.tensor_scalar(out=h_64[:], in0=h_n2[:], scalar1=64.0, scalar2=1.0, op0=ALU.mult, op1=ALU.mult)

        live = {}

        def tokens(c):
            return CHUNK_ROWS[c] * P

        def x_turn(c):
            if c in DMA_LAID:
                return
            banks = []
            for b in range(0, CHUNK_ROWS[c], 2):
                qs = [FIRST_ROW[c] + b + k for k in range(min(2, CHUNK_ROWS[c] - b))]
                banks.append((b, len(qs), turn([(x_sb[q // 2], q % 2) for q in qs])))
            live["xt", c] = banks

        def x_lay(c, gain_chunk=None):
            if c in DMA_LAID:
                live["xg", c] = live_laid[c]
                return
            x_g = work.tile([P, PACK * tokens(c)], BF16, name="x_g", tag="x_g", align_bytes=64)
            for first, n, bank in (reversed(live["xt", c]) if XLAY_REVERSED else live["xt", c]):
                lay(nc.scalar.copy, x_g, first, n, bank)
                if gain_chunk is not None and first == 0:
                    gain_of(gain_chunk)
            live["xg", c] = x_g

        def x_quant(c):
            x_q = work.tile([P, tokens(c)], U32, name="x_q", tag="x_q", align_bytes=64, bufs=3 + LEAD)
            x_s = work.tile([P, tokens(c)], U8, name="x_s", tag="x_s", align_bytes=64, bufs=3 + LEAD)
            nc.vector.quantize_mx(out=x_q[:].bitcast(FP8X4), scales=x_s[:], in_=live["xg", c][:])
            live["xq", c] = (x_q, x_s)

        def stage1(c):
            x_q, x_s = live["xq", c]
            banks = []
            for t in range(PACK):
                if t % 2 == 0:
                    banks.append(psum.tile([P, 2, tokens(c)], STAGE1_BANK, name="sum1", tag="bank"))
                nc.tensor.matmul_mx(
                    out=banks[t // 2][:, t % 2, :],
                    lhsT=w1_q[:, t * P : (t + 1) * P].bitcast(FP8X4),
                    lhsT_scale=w1_s[:, t * P : (t + 1) * P],
                    rhs=x_q[:].bitcast(FP8X4),
                    rhs_scale=x_s[:],
                    start=True,
                    stop=True,
                )
            live["s1", c] = banks
            live["a", c] = work.tile([P, PACK, tokens(c)], BF16, name="a_rows", tag="a_rows")

        def read1_scalar(c, t):
            nc.scalar.activation(
                out=live["a", c][:, t, :], in_=live["s1", c][t // 2][:, t % 2, :], func=ACT.Relu, bias=b1_sb[:, t : t + 1], scale=1.0
            )

        def vector_pieces(c):
            if VK1_EVERY and CHUNK_ROWS[c] == 4 and c % VK1_EVERY == VK1_EVERY - 1:
                return 1
            if c in VK1_CHUNKS:
                return 1
            return 3 if (VK3_EVERY and CHUNK_ROWS[c] == 4 and c % VK3_EVERY == VK3_EVERY - 1) else 2

        def read1_vector_one(c, t):
            nc.vector.tensor_scalar(
                out=live["a", c][:, t, :], in0=live["s1", c][t // 2][:, t % 2, :], scalar1=b1_sb[:, t : t + 1], scalar2=0.0,
                op0=ALU.add, op1=ALU.max,
            )

        def read1_vector_pair(c):
            nc.vector.tensor_tensor(
                out=live["a", c][:, 2:4, :], in0=live["s1", c][1][:], in1=b1_wide[:, :, 0 : tokens(c)], op=ALU.add
            )

        def a_lay(c):
            a_g = work.tile([P, PACK * tokens(c)], BF16, name="a_g", tag="a_g", align_bytes=64)
            nc.vector.tensor_scalar_max(
                out=a_g[:].rearrange("p (c i t) -> p c t i", i=RUN, t=PACK),
                in0=live["a", c][:].rearrange("p t (c i) -> p c t i", i=RUN),
                scalar1=0.0,
            )
            live["ag", c] = a_g

        def a_quant(c):
            a_q = work.tile([P, tokens(c)], U32, name="a_q", tag="a_q", align_bytes=64)
            a_s = work.tile([P, tokens(c)], U8, name="a_s", tag="a_s", align_bytes=64)
            nc.vector.quantize_mx(out=a_q[:].bitcast(FP8X4), scales=a_s[:], in_=live["ag", c][:])
            live["aq", c] = (a_q, a_s)

        def stage2(c):
            a_q, a_s = live["aq", c]
            bank = psum.tile([P, tokens(c)], F32, name="sum2", tag="bank")
            nc.tensor.matmul_mx(
                out=bank[:],
                lhsT=w2_q[:].bitcast(FP8X4),
                lhsT_scale=w2_s[:],
                rhs=a_q[:].bitcast(FP8X4),
                rhs_scale=a_s[:],
                start=True,
                stop=True,
            )
            live["z", c] = bank

        def u_read(c):
            u_t = work.tile([P, tokens(c)], F32, name="u_t", tag="u_t")
            nc.scalar.activation(out=u_t[:], in_=live["z", c][:], func=ACT.Identity, bias=b2_sb[:, 0:1], scale=1.0)
            live["u", c] = u_t

        def rotate(c):
            bank = psum.tile([P, tokens(c)], F32, name="v_rows", tag="bank")
            for r in range(CHUNK_ROWS[c]):
                nc.tensor.matmul(
                    out=bank[:, r * P : (r + 1) * P], lhsT=live["u", c][:, r * P : (r + 1) * P], rhs=tap[:], start=True, stop=True
                )
            live["v", c] = bank

        def norms(c):
            sq_sum = work.tile([P, CHUNK_ROWS[c]], F32, name="sq_sum", tag="sq_sum")
            for r in range(CHUNK_ROWS[c]):
                squares = work.tile([P, P], BF16, name="squares", tag="squares")
                nc.scalar.activation(
                    out=squares[:], in_=live["v", c][:, r * P : (r + 1) * P], func=ACT.Square, accum_out=sq_sum[:, r : r + 1]
                )
            live["sq", c] = sq_sum
            if not DEFER_GAIN:
                gain_of(c)

        def gain_of(c):
            gain = work.tile([P, CHUNK_ROWS[c]], F32, name="gain", tag="gain")
            nc.scalar.activation(out=gain[:], in_=live["sq", c][:], func=ACT.Abs_reciprocal_sqrt, scale=inv_c[:, 0:1])
            live["gain", c] = gain

        def finish(c):
            y = yout.tile([P, tokens(c)], F32, name="y", tag="y")
            for r in range(CHUNK_ROWS[c]):
                q = FIRST_ROW[c] + r
                first = q % (NROWS // NGRP) * P
                nc.vector.scalar_tensor_tensor(
                    out=y[:, r * P : (r + 1) * P],
                    in0=live["v", c][:, r * P : (r + 1) * P],
                    scalar=live["gain", c][:, r : r + 1],
                    in1=n_sb[q // (NROWS // NGRP)][:, first : first + P],
                    op0=ALU.mult,
                    op1=ALU.add,
                )
            nc.sync.dma_start(out=o_v[:, FIRST_ROW[c] * P : (FIRST_ROW[c] + CHUNK_ROWS[c]) * P], in_=y[:])

        def on(c):
            return 0 <= c < NCH

        for i in range(NCH + DEPTH):
            gain_due = on(i - 5)
            pair_first = PAIR_FIRST and not (HYBRID and on(i) and on(i - 5))
            if i == 0:
                x_turn(0)
                keep_warm(WARM[2])
                if not W2_BEHIND:
                    live["w2t"] = turn([(w2_raw, 0)])
                    keep_warm(WARM[3])
            if on(i):
                if GAIN_BETWEEN and gain_due:
                    x_lay(i, i - 5)
                    gain_due = False
                else:
                    x_lay(i)
                x_quant(i)
                if gain_due:
                    gain_of(i - 5)
                    gain_due = False
            if i == (1 if W2_BEHIND else 0):
                lay_w2()
            if i == 1:
                quantize_w2()
            if not pair_first and on(i - 2):
                a_quant(i - 2)
            if on(i - 1):
                stage1(i - 1)
                for t in range(4 - vector_pieces(i - 1)):
                    read1_scalar(i - 1, t)
                if gain_due:
                    gain_of(i - 5)
                    gain_due = False
                if vector_pieces(i - 1) == 3:
                    read1_vector_one(i - 1, 1)
                if vector_pieces(i - 1) == 1:
                    read1_vector_one(i - 1, 3)
                else:
                    read1_vector_pair(i - 1)
            if pair_first and on(i - 2):
                a_quant(i - 2)
            early_u = gain_due and on(i - 3)
            if early_u:
                stage2(i - 3)
                u_read(i - 3)
            if gain_due:
                gain_of(i - 5)
            if FINISH_LAST and on(i - 1):
                a_lay(i - 1)
            if on(i - 5):
                finish(i - 5)
            if not FINISH_LAST and on(i - 1):
                a_lay(i - 1)
            if on(i - 3) and not early_u:
                stage2(i - 3)
                u_read(i - 3)
            if on(i - 4):
                rotate(i - 4)
            if TURN_EACH:
                if on(i + 1):
                    x_turn(i + 1)
                if W2_BEHIND and i == 0:
                    live["w2t"] = turn([(w2_raw, 0)])
                    keep_warm(WARM[3])
            elif i % 2 == 0:
                for c in (i + 1, i + 2):
                    if on(c):
                        x_turn(c)
            if on(i - 4):
                norms(i - 4)
